import numpy as np
import ml_dtypes


def mxq(x, axis, fmt="e4m3"):
    dtype, down = {"e4m3": (ml_dtypes.float8_e4m3fn, 7), "e5m2": (ml_dtypes.float8_e5m2, 14)}[fmt]
    v = np.moveaxis(np.asarray(x, np.float32).astype(ml_dtypes.bfloat16).astype(np.float64), axis, -1)
    blocks = v.reshape(v.shape[:-1] + (-1, 32))
    amax = np.abs(blocks).max(-1, keepdims=True)
    byte = np.maximum(np.where(amax > 0, np.frexp(amax)[1] - 1 + 127, 0) - down, 1)
    scale = np.exp2(byte - 127.0)
    codes = (blocks / scale).astype(np.float32).astype(dtype).astype(np.float64)
    return np.moveaxis((codes * scale).reshape(v.shape), -1, axis)


WIDE = False


def mx_kscale(k):
    if not WIDE:
        return np.ones(k)
    levels = np.array([10, -10, 5, -5, 0])
    a = np.random.permutation(np.resize(levels, k // 512 * 4)).reshape(k // 512, 4)
    idx = np.arange(k)
    return np.exp2(a[idx // 512, idx % 128 // 32])


BF16 = ml_dtypes.bfloat16


def bf(x):
    return np.asarray(x, np.float32).astype(BF16)


def f64(x):
    return np.asarray(x).astype(np.float64)


E2M1 = np.array([0.0, 0.5, 1.0, 1.5, 2.0, 3.0, 4.0, 6.0, -0.0, -0.5, -1.0, -1.5, -2.0, -3.0, -4.0, -6.0])


def pack_weight(w, fmt):
    k, n = w.shape
    w = f64(bf(w)).reshape(k // 32, 32, n)
    amax = np.abs(w).max(1)
    if fmt == "e4m3":
        byte = np.frexp(amax)[1] - 1 + 127 - 7
    else:
        mant, ex = np.frexp(amax / 6.0)
        byte = np.where(mant > 0.5, ex, ex - 1) + 127
    byte = np.clip(np.where(amax > 0, byte, 1), 1, 254)
    scaled = (w * np.exp2(127.0 - byte)[:, None, :]).reshape(k, n).astype(np.float32)
    by_word = np.ascontiguousarray(scaled.reshape(k // 512, 128, 4, n).transpose(0, 1, 3, 2))
    if fmt == "e4m3":
        words = by_word.astype(ml_dtypes.float8_e4m3fn).view(np.uint8)
    else:
        c = by_word.astype(ml_dtypes.float4_e2m1fn).view(np.uint8) & 0xF
        words = c[..., 0::2] | (c[..., 1::2] << 4)
    return np.ascontiguousarray(words), np.ascontiguousarray(byte.astype(np.uint8).reshape(k // 512, 16, n))


def unpack_weight(words, scales, fmt):
    g, p, n, _ = words.shape
    if fmt == "e4m3":
        vals = np.ascontiguousarray(words).view(ml_dtypes.float8_e4m3fn).astype(np.float64)
    else:
        nib = np.empty((g, p, n, 4), np.uint8)
        nib[..., 0::2] = words & 0xF
        nib[..., 1::2] = words >> 4
        vals = E2M1[nib]
    vals = vals * np.repeat(np.exp2(scales.astype(np.float64) - 127.0), 8, axis=1)[..., None]
    return vals.transpose(0, 1, 3, 2).reshape(g * 512, n)


B, E, D = 4096, 512, 512
FMT = "e4m3"


def hard_sigmoid(z):
    return np.clip(z / 6.0 + 0.5, 0.0, 1.0)


def setup_inputs():
    s = mx_kscale(E)
    t = mx_kscale(D)
    x = bf(np.random.standard_normal((B, E)) * s)
    state_x = bf(np.random.standard_normal((B, E)) * s)
    time_mix_r = bf(np.random.uniform(0.0, 1.0, (1, E)))
    w_r = np.random.standard_normal((D, E)) * 3.5 / np.sqrt(E) / s[None, :]
    wr_words, wr_scales = pack_weight(np.ascontiguousarray(w_r.T), FMT)
    wkv_num = bf((0.5 + 0.5 * np.random.standard_normal((B, D))) * t)
    wkv_den = bf(0.5 + 1.5 * np.random.uniform(0.0, 1.0, (B, D)))
    w_o = np.random.standard_normal((E, D)) * 2.0 / np.sqrt(D) / t[None, :]
    wo_words, wo_scales = pack_weight(np.ascontiguousarray(w_o.T), FMT)
    return {
        "x": x,
        "state_x": state_x,
        "time_mix_r": time_mix_r,
        "W_receptance_words": wr_words,
        "W_receptance_scales": wr_scales,
        "wkv_num": wkv_num,
        "wkv_den": wkv_den,
        "W_output_words": wo_words,
        "W_output_scales": wo_scales,
    }


def reference(x, state_x, time_mix_r, W_receptance_words, W_receptance_scales, wkv_num, wkv_den, W_output_words, W_output_scales):
    x, state_x, mr = f64(x), f64(state_x), f64(time_mix_r)
    xr = x * mr + state_x * (1.0 - mr)
    r = hard_sigmoid(mxq(xr, 1, "e4m3") @ unpack_weight(W_receptance_words, W_receptance_scales, FMT))
    h = r * f64(wkv_num) / f64(wkv_den)
    return mxq(h, 1, "e4m3") @ unpack_weight(W_output_words, W_output_scales, FMT)

@@ -1,0 +1,309 @@
+from contextlib import ExitStack
+
+import concourse.mybir as mybir
+from concourse.masks import make_identity
+
+F32 = mybir.dt.float32
+BF16 = mybir.dt.bfloat16
+I32 = mybir.dt.int32
+U8 = mybir.dt.uint8
+U32 = mybir.dt.uint32
+FP8X4 = mybir.dt.float8_e4m3fn_x4
+ACT = mybir.ActivationFunctionType
+ALU = mybir.AluOpType
+
+P = 128
+PACK = 4
+HALVES = 2
+WORDS = PACK // HALVES
+ROWS = 4096
+WIDTH = 512
+GROUP_TILES = 2
+GROUP_ROWS = GROUP_TILES * P
+GROUPS = ROWS // GROUP_ROWS
+CHUNK_TILES = 4
+CHUNK_ROWS = CHUNK_TILES * P
+CHUNKS = ROWS // CHUNK_ROWS
+CHUNKS_AHEAD = 2
+SCALE_ROWS = 16
+
+FLOPS = 2 * 2 * ROWS * WIDTH * WIDTH
+
+
+def tile_rwkv_timemix_for_quant_pb_t_kernel(
+    tc,
+    x,
+    state_x,
+    time_mix_r,
+    W_receptance_words,
+    W_receptance_scales,
+    wkv_num,
+    wkv_den,
+    W_output_words,
+    W_output_scales,
+    out,
+):
+    nc = tc.nc
+    with ExitStack() as ctx:
+        consts = ctx.enter_context(tc.tile_pool(name="consts", bufs=1))
+        inputs = ctx.enter_context(tc.tile_pool(name="inputs", bufs=4))
+        work = ctx.enter_context(tc.tile_pool(name="work", bufs=2))
+        results = ctx.enter_context(tc.tile_pool(name="results", bufs=3))
+        words_psum = ctx.enter_context(tc.psum_pool(name="words_psum", bufs=1))
+        gate_psum = ctx.enter_context(tc.psum_pool(name="gate_psum", bufs=3))
+        out_psum = ctx.enter_context(tc.psum_pool(name="out_psum", bufs=2))
+        ctx.enter_context(tc.manual_schedule())
+
+        sx_of, x_of, den_of, num_of = {}, {}, {}, {}
+        sxw_of, xw_of, denw_of = {}, {}, {}
+        xr_planes_of, xr_grouped_of, xr_codes_of, xr_scales_of = {}, {}, {}, {}
+        z_of, lower_of, gated_of, gated_t_of = {}, {}, {}, {}
+        rsqrt_of, rden_of = {}, {}
+        h_grouped_of, h_codes_of, h_scales_of, o_of = {}, {}, {}, {}
+
+        def chunk_view(dram, c):
+            rows = dram[c * CHUNK_ROWS : (c + 1) * CHUNK_ROWS, :]
+            return rows.rearrange("(p r) e -> p r e", r=CHUNK_TILES)
+
+        def load_chunk(c):
+            sx_sb = inputs.tile([P, CHUNK_TILES, WIDTH], BF16)
+            nc.sync.dma_start(out=sx_sb[:], in_=chunk_view(state_x, c))
+            x_sb = inputs.tile([P, CHUNK_TILES, WIDTH], BF16)
+            nc.sync.dma_start(out=x_sb[:], in_=chunk_view(x, c))
+            den_sb = inputs.tile([P, CHUNK_TILES, WIDTH], BF16)
+            nc.sync.dma_start(out=den_sb[:], in_=chunk_view(wkv_den, c))
+            num_sb = inputs.tile([P, CHUNK_TILES, WIDTH], BF16)
+            nc.sync.dma_start(out=num_sb[:], in_=chunk_view(wkv_num, c))
+            sx_of[c], x_of[c], den_of[c], num_of[c] = sx_sb, x_sb, den_sb, num_sb
+
+        def load_weight(words, scales, label):
+            codes = consts.tile([P, PACK * WIDTH], U8, name=label + "_codes", align_bytes=64)
+            nc.sync.dma_start(
+                out=codes[:].bitcast(I32),
+                in_=words[0].rearrange("p n t -> p (n t)").bitcast(I32),
+            )
+            plane = consts.tile([P, WIDTH], U8, name=label + "_plane", align_bytes=64)
+            nc.vector.memset(plane[:].bitcast(I32), 0)
+            for quadrant in range(SCALE_ROWS // PACK):
+                nc.sync.dma_start(
+                    out=plane[32 * quadrant : 32 * quadrant + PACK, :].bitcast(I32),
+                    in_=scales[0, PACK * quadrant : PACK * (quadrant + 1), :].bitcast(I32),
+                )
+            return codes, plane
+
+        def row_tile(g, j):
+            return g // (CHUNK_TILES // GROUP_TILES), (g % (CHUNK_TILES // GROUP_TILES)) * GROUP_TILES + j
+
+        def half_of_words(bank, u, e):
+            return bank[:, u, :].bitcast(BF16).rearrange("p (b e) -> p b e", e=HALVES)[:, :, e]
+
+        def transpose_words(g, source_of, bank):
+            for j in range(GROUP_TILES):
+                c, r = row_tile(g, j)
+                as_words = source_of[c][:, r, :].bitcast(F32)
+                for u in range(WORDS):
+                    nc.tensor.transpose(
+                        bank[:, u, j * P : (j + 1) * P],
+                        as_words[:, u : WIDTH // HALVES : WORDS],
+                        identity[:],
+                    )
+
+        def transpose_inputs(g):
+            sxw = words_psum.tile([P, WORDS, GROUP_ROWS], F32)
+            transpose_words(g, sx_of, sxw)
+            xw = words_psum.tile([P, WORDS, GROUP_ROWS], F32)
+            transpose_words(g, x_of, xw)
+            denw = words_psum.tile([P, WORDS, GROUP_ROWS], F32)
+            transpose_words(g, den_of, denw)
+            sxw_of[g], xw_of[g], denw_of[g] = sxw, xw, denw
+
+        def mix(g):
+            kept = work.tile([P, PACK, GROUP_ROWS], F32)
+            xr_planes = work.tile([P, PACK, GROUP_ROWS], BF16)
+            for u in range(WORDS):
+                for e in range(HALVES):
+                    t = HALVES * u + e
+                    nc.scalar.activation(
+                        out=kept[:, t, :],
+                        in_=half_of_words(sxw_of[g], u, e),
+                        func=ACT.Copy,
+                        scale=one_minus_mix[:, t : t + 1],
+                    )
+                    nc.vector.scalar_tensor_tensor(
+                        out=xr_planes[:, t, :],
+                        in0=half_of_words(xw_of[g], u, e),
+                        scalar=mix_r[:, t : t + 1],
+                        in1=kept[:, t, :],
+                        op0=ALU.mult,
+                        op1=ALU.add,
+                    )
+            xr_planes_of[g] = xr_planes
+
+        def regroup_xr(g):
+            xr_grouped = work.tile([P, GROUP_ROWS, PACK], BF16, align_bytes=64)
+            nc.vector.tensor_copy(
+                out=xr_grouped[:], in_=xr_planes_of[g][:].rearrange("p t b -> p b t")
+            )
+            xr_grouped_of[g] = xr_grouped
+
+        def quantise(grouped, codes, scales):
+            nc.vector.quantize_mx(
+                out=codes[:].bitcast(FP8X4),
+                scales=scales[:],
+                in_=grouped[:].rearrange("p b t -> p (b t)"),
+            )
+
+        def quantise_xr(g):
+            xr_codes = work.tile([P, GROUP_ROWS], U32, align_bytes=64)
+            xr_scales = work.tile([P, GROUP_ROWS], U8, align_bytes=64)
+            quantise(xr_grouped_of[g], xr_codes, xr_scales)
+            xr_codes_of[g], xr_scales_of[g] = xr_codes, xr_scales
+
+        def quantise_h(g):
+            h_codes = work.tile([P, GROUP_ROWS], U32, align_bytes=64)
+            h_scales = work.tile([P, GROUP_ROWS], U8, align_bytes=64)
+            quantise(h_grouped_of[g], h_codes, h_scales)
+            h_codes_of[g], h_scales_of[g] = h_codes, h_scales
+
+        def one_pass(acc, codes, scales, j, weight_codes, weight_plane):
+            nc.tensor.matmul_mx(
+                out=acc[:],
+                lhsT=codes[:, j * P : (j + 1) * P].bitcast(FP8X4),
+                lhsT_scale=scales[:, j * P : (j + 1) * P],
+                rhs=weight_codes[:].bitcast(FP8X4),
+                rhs_scale=weight_plane[:],
+                start=True,
+                stop=True,
+            )
+
+        def receptance_matmul(g):
+            for j in range(GROUP_TILES):
+                z = gate_psum.tile([P, WIDTH], F32, tag="gate")
+                one_pass(z, xr_codes_of[g], xr_scales_of[g], j, wr_codes, wr_plane)
+                z_of[g, j] = z
+
+        def output_matmul(g):
+            for j in range(GROUP_TILES):
+                o = out_psum.tile([P, WIDTH], F32)
+                one_pass(o, h_codes_of[g], h_scales_of[g], j, wo_codes, wo_plane)
+                o_of[g, j] = o
+
+        def clip_below(g):
+            lower = work.tile([P, GROUP_TILES, WIDTH], F32)
+            for j in range(GROUP_TILES):
+                nc.scalar.activation(
+                    out=lower[:, j, :], in_=z_of[g, j][:], func=ACT.Relu, scale=1.0 / 6.0, bias=half[:]
+                )
+            lower_of[g] = lower
+
+        def gate_num(g):
+            gated = work.tile([P, GROUP_TILES, PACK, P], F32)
+            for j in range(GROUP_TILES):
+                c, r = row_tile(g, j)
+                nc.vector.scalar_tensor_tensor(
+                    out=gated[:, j, :, :],
+                    in0=lower_of[g][:, j, :].rearrange("b (p t) -> b t p", t=PACK),
+                    scalar=1.0,
+                    in1=num_of[c][:, r, :].rearrange("b (p t) -> b t p", t=PACK),
+                    op0=ALU.min,
+                    op1=ALU.mult,
+                )
+            gated_of[g] = gated
+
+        def transpose_gated(g):
+            for j in range(GROUP_TILES):
+                gated_t = gate_psum.tile([P, PACK, P], F32, tag="gate")
+                for t in range(PACK):
+                    nc.tensor.transpose(gated_t[:, t, :], gated_of[g][:, j, t, :], identity[:])
+                gated_t_of[g, j] = gated_t
+
+        def rsqrt_den(g):
+            rsqrt = work.tile([P, GROUP_ROWS, WORDS, HALVES], F32)
+            halves = denw_of[g][:].rearrange("p u b -> p (u b)").bitcast(BF16)
+            nc.scalar.activation(
+                out=rsqrt[:],
+                in_=halves.rearrange("p (u b e) -> p b u e", u=WORDS, e=HALVES),
+                func=ACT.Abs_reciprocal_sqrt,
+            )
+            rsqrt_of[g] = rsqrt
+
+        def square_rsqrt(g):
+            rden = results.tile([P, GROUP_ROWS, PACK], F32)
+            nc.scalar.activation(
+                out=rden[:], in_=rsqrt_of[g][:].rearrange("p b u e -> p b (u e)"), func=ACT.Square
+            )
+            rden_of[g] = rden
+
+        def divide(g):
+            h_grouped = work.tile([P, GROUP_ROWS, PACK], BF16, align_bytes=64)
+            for j in range(GROUP_TILES):
+                nc.vector.tensor_tensor(
+                    out=h_grouped[:, j * P : (j + 1) * P, :],
+                    in0=gated_t_of[g, j][:].rearrange("p t b -> p b t"),
+                    in1=rden_of[g][:, j * P : (j + 1) * P, :],
+                    op=ALU.mult,
+                )
+            h_grouped_of[g] = h_grouped
+
+        def store_out(g):
+            out_sb = results.tile([P, GROUP_TILES, WIDTH], F32)
+            nc.scalar.copy(out=out_sb[:, 0, :], in_=o_of[g, 0][:])
+            nc.vector.tensor_copy(out=out_sb[:, 1, :], in_=o_of[g, 1][:])
+            c, r = row_tile(g, 0)
+            nc.sync.dma_start(out=chunk_view(out, c)[:, r : r + GROUP_TILES, :], in_=out_sb[:])
+
+        mix_bf = consts.tile([P, PACK], BF16)
+        nc.sync.dma_start(out=mix_bf[:], in_=time_mix_r[0].rearrange("(p t) -> p t", t=PACK))
+        load_chunk(0)
+        wr_codes, wr_plane = load_weight(W_receptance_words, W_receptance_scales, "wr")
+        wo_codes, wo_plane = load_weight(W_output_words, W_output_scales, "wo")
+        for c in range(1, CHUNKS_AHEAD):
+            load_chunk(c)
+
+        identity = consts.tile([P, P], F32)
+        make_identity(nc, identity[:])
+        half = consts.tile([P, 1], F32)
+        nc.vector.memset(half[:], 0.5)
+        mix_r = consts.tile([P, PACK], F32)
+        nc.vector.tensor_copy(out=mix_r[:], in_=mix_bf[:])
+        one_minus_mix = consts.tile([P, PACK], F32)
+        nc.vector.tensor_scalar(
+            out=one_minus_mix[:], in0=mix_bf[:], scalar1=-1.0, scalar2=1.0, op0=ALU.mult, op1=ALU.add
+        )
+
+        def live(g):
+            return 0 <= g < GROUPS
+
+        for turn in range(-2, GROUPS + 1):
+            if live(turn):
+                quantise_xr(turn)
+            if live(turn - 1):
+                quantise_h(turn - 1)
+            if live(turn):
+                receptance_matmul(turn)
+            if live(turn - 1):
+                output_matmul(turn - 1)
+            if live(turn + 1):
+                mix(turn + 1)
+            if live(turn):
+                clip_below(turn)
+            if live(turn + 1):
+                rsqrt_den(turn + 1)
+            if live(turn - 1):
+                store_out(turn - 1)
+            if live(turn):
+                gate_num(turn)
+            if live(turn + 1):
+                square_rsqrt(turn + 1)
+            if live(turn):
+                transpose_gated(turn)
+            if live(turn + 2):
+                if (turn + 2) % (CHUNK_TILES // GROUP_TILES) == 0:
+                    ahead = (turn + 2) // (CHUNK_TILES // GROUP_TILES) + CHUNKS_AHEAD
+                    if ahead < CHUNKS:
+                        load_chunk(ahead)
+                transpose_inputs(turn + 2)
+            if live(turn + 1):
+                regroup_xr(turn + 1)
+            if live(turn):
+                divide(turn)

@@ -274,29 +274,29 @@ def tile_rwkv_timemix_for_quant_pb_t_kernel(
         def live(g):
             return 0 <= g < GROUPS
 
-        for turn in range(-2, GROUPS + 1):
+        for turn in range(-2, GROUPS + 2):
             if live(turn):
                 quantise_xr(turn)
-            if live(turn - 1):
-                quantise_h(turn - 1)
+            if live(turn - 2):
+                quantise_h(turn - 2)
             if live(turn):
                 receptance_matmul(turn)
+            if live(turn - 2):
+                output_matmul(turn - 2)
             if live(turn - 1):
-                output_matmul(turn - 1)
+                gate_num(turn - 1)
             if live(turn + 1):
                 mix(turn + 1)
             if live(turn):
                 clip_below(turn)
             if live(turn + 1):
                 rsqrt_den(turn + 1)
-            if live(turn - 1):
-                store_out(turn - 1)
-            if live(turn):
-                gate_num(turn)
+            if live(turn - 2):
+                store_out(turn - 2)
             if live(turn + 1):
                 square_rsqrt(turn + 1)
-            if live(turn):
-                transpose_gated(turn)
+            if live(turn - 1):
+                transpose_gated(turn - 1)
             if live(turn + 2):
                 if (turn + 2) % (CHUNK_TILES // GROUP_TILES) == 0:
                     ahead = (turn + 2) // (CHUNK_TILES // GROUP_TILES) + CHUNKS_AHEAD
@@ -305,5 +305,5 @@ def tile_rwkv_timemix_for_quant_pb_t_kernel(
                 transpose_inputs(turn + 2)
             if live(turn + 1):
                 regroup_xr(turn + 1)
-            if live(turn):
-                divide(turn)
+            if live(turn - 1):
+                divide(turn - 1)

@@ -201,10 +201,10 @@ def tile_rwkv_timemix_for_quant_pb_t_kernel(
             for j in range(GROUP_TILES):
                 c, r = row_tile(g, j)
                 nc.vector.scalar_tensor_tensor(
-                    out=gated[:, j, :, :],
-                    in0=lower_of[g][:, j, :].rearrange("b (p t) -> b t p", t=PACK),
+                    out=gated[:, j, :, :].rearrange("b t p -> b p t"),
+                    in0=lower_of[g][:, j, :].rearrange("b (p t) -> b p t", t=PACK),
                     scalar=1.0,
-                    in1=num_of[c][:, r, :].rearrange("b (p t) -> b t p", t=PACK),
+                    in1=num_of[c][:, r, :].rearrange("b (p t) -> b p t", t=PACK),
                     op0=ALU.min,
                     op1=ALU.mult,
                 )

@@ -141,8 +141,13 @@ def tile_rwkv_timemix_for_quant_pb_t_kernel(
 
         def regroup_xr(g):
             xr_grouped = work.tile([P, GROUP_ROWS, PACK], BF16, align_bytes=64)
-            nc.vector.tensor_copy(
-                out=xr_grouped[:], in_=xr_planes_of[g][:].rearrange("p t b -> p b t")
+            nc.gpsimd.tensor_scalar(
+                out=xr_grouped[:],
+                in0=xr_planes_of[g][:].rearrange("p t b -> p b t"),
+                scalar1=1.0,
+                scalar2=0.0,
+                op0=ALU.mult,
+                op1=ALU.add,
             )
             xr_grouped_of[g] = xr_grouped
 
@@ -275,24 +280,24 @@ def tile_rwkv_timemix_for_quant_pb_t_kernel(
             return 0 <= g < GROUPS
 
         for turn in range(-2, GROUPS + 2):
+            if live(turn - 2):
+                quantise_h(turn - 2)
+            if live(turn - 1):
+                gate_num(turn - 1)
             if live(turn):
                 quantise_xr(turn)
             if live(turn - 2):
-                quantise_h(turn - 2)
+                output_matmul(turn - 2)
             if live(turn):
                 receptance_matmul(turn)
-            if live(turn - 2):
-                output_matmul(turn - 2)
-            if live(turn - 1):
-                gate_num(turn - 1)
             if live(turn + 1):
                 mix(turn + 1)
-            if live(turn):
-                clip_below(turn)
-            if live(turn + 1):
+                regroup_xr(turn + 1)
                 rsqrt_den(turn + 1)
             if live(turn - 2):
                 store_out(turn - 2)
+            if live(turn):
+                clip_below(turn)
             if live(turn + 1):
                 square_rsqrt(turn + 1)
             if live(turn - 1):
@@ -303,7 +308,5 @@ def tile_rwkv_timemix_for_quant_pb_t_kernel(
                     if ahead < CHUNKS:
                         load_chunk(ahead)
                 transpose_inputs(turn + 2)
-            if live(turn + 1):
-                regroup_xr(turn + 1)
             if live(turn - 1):
                 divide(turn - 1)

@@ -21,11 +21,9 @@ WIDTH = 512
 GROUP_TILES = 2
 GROUP_ROWS = GROUP_TILES * P
 GROUPS = ROWS // GROUP_ROWS
-CHUNK_TILES = 4
-CHUNK_ROWS = CHUNK_TILES * P
-CHUNKS = ROWS // CHUNK_ROWS
-CHUNKS_AHEAD = 2
+GROUPS_AHEAD = 3
 SCALE_ROWS = 16
+RUN = 4
 
 FLOPS = 2 * 2 * ROWS * WIDTH * WIDTH
 
@@ -46,9 +44,9 @@ def tile_rwkv_timemix_for_quant_pb_t_kernel(
     nc = tc.nc
     with ExitStack() as ctx:
         consts = ctx.enter_context(tc.tile_pool(name="consts", bufs=1))
-        inputs = ctx.enter_context(tc.tile_pool(name="inputs", bufs=4))
-        work = ctx.enter_context(tc.tile_pool(name="work", bufs=2))
-        results = ctx.enter_context(tc.tile_pool(name="results", bufs=3))
+        inputs = ctx.enter_context(tc.tile_pool(name="inputs", bufs=GROUPS_AHEAD + 2))
+        late_inputs = ctx.enter_context(tc.tile_pool(name="late_inputs", bufs=GROUPS_AHEAD + 5))
+        work = ctx.enter_context(tc.tile_pool(name="work", bufs=3))
         words_psum = ctx.enter_context(tc.psum_pool(name="words_psum", bufs=1))
         gate_psum = ctx.enter_context(tc.psum_pool(name="gate_psum", bufs=3))
         out_psum = ctx.enter_context(tc.psum_pool(name="out_psum", bufs=2))
@@ -56,25 +54,25 @@ def tile_rwkv_timemix_for_quant_pb_t_kernel(
 
         sx_of, x_of, den_of, num_of = {}, {}, {}, {}
         sxw_of, xw_of, denw_of = {}, {}, {}
-        xr_planes_of, xr_grouped_of, xr_codes_of, xr_scales_of = {}, {}, {}, {}
+        kept_of, xr_planes_of, xr_grouped_of, xr_codes_of, xr_scales_of = {}, {}, {}, {}, {}
         z_of, lower_of, gated_of, gated_t_of = {}, {}, {}, {}
         rsqrt_of, rden_of = {}, {}
         h_grouped_of, h_codes_of, h_scales_of, o_of = {}, {}, {}, {}
 
-        def chunk_view(dram, c):
-            rows = dram[c * CHUNK_ROWS : (c + 1) * CHUNK_ROWS, :]
-            return rows.rearrange("(p r) e -> p r e", r=CHUNK_TILES)
+        def group_view(dram, g):
+            rows = dram[g * GROUP_ROWS : (g + 1) * GROUP_ROWS, :]
+            return rows.rearrange("(p j) e -> p j e", j=GROUP_TILES)
 
-        def load_chunk(c):
-            sx_sb = inputs.tile([P, CHUNK_TILES, WIDTH], BF16)
-            nc.sync.dma_start(out=sx_sb[:], in_=chunk_view(state_x, c))
-            x_sb = inputs.tile([P, CHUNK_TILES, WIDTH], BF16)
-            nc.sync.dma_start(out=x_sb[:], in_=chunk_view(x, c))
-            den_sb = inputs.tile([P, CHUNK_TILES, WIDTH], BF16)
-            nc.sync.dma_start(out=den_sb[:], in_=chunk_view(wkv_den, c))
-            num_sb = inputs.tile([P, CHUNK_TILES, WIDTH], BF16)
-            nc.sync.dma_start(out=num_sb[:], in_=chunk_view(wkv_num, c))
-            sx_of[c], x_of[c], den_of[c], num_of[c] = sx_sb, x_sb, den_sb, num_sb
+        def load_group(g):
+            sx_sb = inputs.tile([P, GROUP_TILES, WIDTH], BF16)
+            nc.sync.dma_start(out=sx_sb[:], in_=group_view(state_x, g))
+            x_sb = inputs.tile([P, GROUP_TILES, WIDTH], BF16)
+            nc.sync.dma_start(out=x_sb[:], in_=group_view(x, g))
+            den_sb = inputs.tile([P, GROUP_TILES, WIDTH], BF16)
+            nc.sync.dma_start(out=den_sb[:], in_=group_view(wkv_den, g))
+            num_sb = late_inputs.tile([P, GROUP_TILES, WIDTH], BF16)
+            nc.sync.dma_start(out=num_sb[:], in_=group_view(wkv_num, g))
+            sx_of[g], x_of[g], den_of[g], num_of[g] = sx_sb, x_sb, den_sb, num_sb
 
         def load_weight(words, scales, label):
             codes = consts.tile([P, PACK * WIDTH], U8, name=label + "_codes", align_bytes=64)
@@ -91,16 +89,12 @@ def tile_rwkv_timemix_for_quant_pb_t_kernel(
                 )
             return codes, plane
 
-        def row_tile(g, j):
-            return g // (CHUNK_TILES // GROUP_TILES), (g % (CHUNK_TILES // GROUP_TILES)) * GROUP_TILES + j
-
         def half_of_words(bank, u, e):
             return bank[:, u, :].bitcast(BF16).rearrange("p (b e) -> p b e", e=HALVES)[:, :, e]
 
-        def transpose_words(g, source_of, bank):
+        def transpose_words(source, bank):
             for j in range(GROUP_TILES):
-                c, r = row_tile(g, j)
-                as_words = source_of[c][:, r, :].bitcast(F32)
+                as_words = source[:, j, :].bitcast(F32)
                 for u in range(WORDS):
                     nc.tensor.transpose(
                         bank[:, u, j * P : (j + 1) * P],
@@ -110,16 +104,15 @@ def tile_rwkv_timemix_for_quant_pb_t_kernel(
 
         def transpose_inputs(g):
             sxw = words_psum.tile([P, WORDS, GROUP_ROWS], F32)
-            transpose_words(g, sx_of, sxw)
+            transpose_words(sx_of[g], sxw)
             xw = words_psum.tile([P, WORDS, GROUP_ROWS], F32)
-            transpose_words(g, x_of, xw)
+            transpose_words(x_of[g], xw)
             denw = words_psum.tile([P, WORDS, GROUP_ROWS], F32)
-            transpose_words(g, den_of, denw)
+            transpose_words(den_of[g], denw)
             sxw_of[g], xw_of[g], denw_of[g] = sxw, xw, denw
 
-        def mix(g):
+        def scale_state(g):
             kept = work.tile([P, PACK, GROUP_ROWS], F32)
-            xr_planes = work.tile([P, PACK, GROUP_ROWS], BF16)
             for u in range(WORDS):
                 for e in range(HALVES):
                     t = HALVES * u + e
@@ -129,11 +122,18 @@ def tile_rwkv_timemix_for_quant_pb_t_kernel(
                         func=ACT.Copy,
                         scale=one_minus_mix[:, t : t + 1],
                     )
+            kept_of[g] = kept
+
+        def mix_in_x(g):
+            xr_planes = work.tile([P, PACK, GROUP_ROWS], BF16)
+            for u in range(WORDS):
+                for e in range(HALVES):
+                    t = HALVES * u + e
                     nc.vector.scalar_tensor_tensor(
                         out=xr_planes[:, t, :],
                         in0=half_of_words(xw_of[g], u, e),
                         scalar=mix_r[:, t : t + 1],
-                        in1=kept[:, t, :],
+                        in1=kept_of[g][:, t, :],
                         op0=ALU.mult,
                         op1=ALU.add,
                     )
@@ -141,13 +141,9 @@ def tile_rwkv_timemix_for_quant_pb_t_kernel(
 
         def regroup_xr(g):
             xr_grouped = work.tile([P, GROUP_ROWS, PACK], BF16, align_bytes=64)
-            nc.gpsimd.tensor_scalar(
-                out=xr_grouped[:],
-                in0=xr_planes_of[g][:].rearrange("p t b -> p b t"),
-                scalar1=1.0,
-                scalar2=0.0,
-                op0=ALU.mult,
-                op1=ALU.add,
+            nc.vector.tensor_copy(
+                out=xr_grouped[:].rearrange("p (c i) t -> p c t i", i=RUN),
+                in_=xr_planes_of[g][:].rearrange("p t (c i) -> p c t i", i=RUN),
             )
             xr_grouped_of[g] = xr_grouped
 
@@ -204,12 +200,11 @@ def tile_rwkv_timemix_for_quant_pb_t_kernel(
         def gate_num(g):
             gated = work.tile([P, GROUP_TILES, PACK, P], F32)
             for j in range(GROUP_TILES):
-                c, r = row_tile(g, j)
                 nc.vector.scalar_tensor_tensor(
                     out=gated[:, j, :, :].rearrange("b t p -> b p t"),
                     in0=lower_of[g][:, j, :].rearrange("b (p t) -> b p t", t=PACK),
                     scalar=1.0,
-                    in1=num_of[c][:, r, :].rearrange("b (p t) -> b p t", t=PACK),
+                    in1=num_of[g][:, j, :].rearrange("b (p t) -> b p t", t=PACK),
                     op0=ALU.min,
                     op1=ALU.mult,
                 )
@@ -233,7 +228,7 @@ def tile_rwkv_timemix_for_quant_pb_t_kernel(
             rsqrt_of[g] = rsqrt
 
         def square_rsqrt(g):
-            rden = results.tile([P, GROUP_ROWS, PACK], F32)
+            rden = work.tile([P, GROUP_ROWS, PACK], F32)
             nc.scalar.activation(
                 out=rden[:], in_=rsqrt_of[g][:].rearrange("p b u e -> p b (u e)"), func=ACT.Square
             )
@@ -251,19 +246,22 @@ def tile_rwkv_timemix_for_quant_pb_t_kernel(
             h_grouped_of[g] = h_grouped
 
         def store_out(g):
-            out_sb = results.tile([P, GROUP_TILES, WIDTH], F32)
+            out_sb = work.tile([P, GROUP_TILES, WIDTH], F32)
             nc.scalar.copy(out=out_sb[:, 0, :], in_=o_of[g, 0][:])
-            nc.vector.tensor_copy(out=out_sb[:, 1, :], in_=o_of[g, 1][:])
-            c, r = row_tile(g, 0)
-            nc.sync.dma_start(out=chunk_view(out, c)[:, r : r + GROUP_TILES, :], in_=out_sb[:])
+            if g % 2 == 1:
+                nc.scalar.copy(out=out_sb[:, 1, :], in_=o_of[g, 1][:])
+            else:
+                nc.vector.tensor_copy(out=out_sb[:, 1, :], in_=o_of[g, 1][:])
+            nc.sync.dma_start(out=group_view(out, g), in_=out_sb[:])
 
         mix_bf = consts.tile([P, PACK], BF16)
         nc.sync.dma_start(out=mix_bf[:], in_=time_mix_r[0].rearrange("(p t) -> p t", t=PACK))
-        load_chunk(0)
+        load_group(0)
         wr_codes, wr_plane = load_weight(W_receptance_words, W_receptance_scales, "wr")
+        load_group(1)
         wo_codes, wo_plane = load_weight(W_output_words, W_output_scales, "wo")
-        for c in range(1, CHUNKS_AHEAD):
-            load_chunk(c)
+        for g in range(2, GROUPS_AHEAD):
+            load_group(g)
 
         identity = consts.tile([P, P], F32)
         make_identity(nc, identity[:])
@@ -279,34 +277,35 @@ def tile_rwkv_timemix_for_quant_pb_t_kernel(
         def live(g):
             return 0 <= g < GROUPS
 
-        for turn in range(-2, GROUPS + 2):
-            if live(turn - 2):
-                quantise_h(turn - 2)
+        for turn in range(-2, GROUPS + 3):
+            if live(turn + 1):
+                scale_state(turn + 1)
             if live(turn - 1):
                 gate_num(turn - 1)
+            if live(turn - 2):
+                quantise_h(turn - 2)
             if live(turn):
                 quantise_xr(turn)
-            if live(turn - 2):
-                output_matmul(turn - 2)
-            if live(turn):
-                receptance_matmul(turn)
             if live(turn + 1):
-                mix(turn + 1)
-                regroup_xr(turn + 1)
                 rsqrt_den(turn + 1)
-            if live(turn - 2):
-                store_out(turn - 2)
-            if live(turn):
-                clip_below(turn)
-            if live(turn + 1):
-                square_rsqrt(turn + 1)
             if live(turn - 1):
                 transpose_gated(turn - 1)
-            if live(turn + 2):
-                if (turn + 2) % (CHUNK_TILES // GROUP_TILES) == 0:
-                    ahead = (turn + 2) // (CHUNK_TILES // GROUP_TILES) + CHUNKS_AHEAD
-                    if ahead < CHUNKS:
-                        load_chunk(ahead)
-                transpose_inputs(turn + 2)
+            if live(turn):
+                receptance_matmul(turn)
+            if live(turn - 2):
+                output_matmul(turn - 2)
             if live(turn - 1):
                 divide(turn - 1)
+            if live(turn - 3):
+                store_out(turn - 3)
+            if live(turn + 1):
+                mix_in_x(turn + 1)
+            if live(turn):
+                clip_below(turn)
+                square_rsqrt(turn)
+            if live(turn + 1):
+                regroup_xr(turn + 1)
+            if live(turn + 2 + GROUPS_AHEAD):
+                load_group(turn + 2 + GROUPS_AHEAD)
+            if live(turn + 2):
+                transpose_inputs(turn + 2)

@@ -45,34 +45,42 @@ def tile_rwkv_timemix_for_quant_pb_t_kernel(
     with ExitStack() as ctx:
         consts = ctx.enter_context(tc.tile_pool(name="consts", bufs=1))
         inputs = ctx.enter_context(tc.tile_pool(name="inputs", bufs=GROUPS_AHEAD + 2))
-        late_inputs = ctx.enter_context(tc.tile_pool(name="late_inputs", bufs=GROUPS_AHEAD + 5))
         work = ctx.enter_context(tc.tile_pool(name="work", bufs=3))
         words_psum = ctx.enter_context(tc.psum_pool(name="words_psum", bufs=1))
-        gate_psum = ctx.enter_context(tc.psum_pool(name="gate_psum", bufs=3))
+        gate_psum = ctx.enter_context(tc.psum_pool(name="gate_psum", bufs=2))
         out_psum = ctx.enter_context(tc.psum_pool(name="out_psum", bufs=2))
         ctx.enter_context(tc.manual_schedule())
 
         sx_of, x_of, den_of, num_of = {}, {}, {}, {}
-        sxw_of, xw_of, denw_of = {}, {}, {}
+        sxw_of, xw_of, denw_of, numw_of = {}, {}, {}, {}
         kept_of, xr_planes_of, xr_grouped_of, xr_codes_of, xr_scales_of = {}, {}, {}, {}, {}
-        z_of, lower_of, gated_of, gated_t_of = {}, {}, {}, {}
+        z_of, lower_of, gated_of = {}, {}, {}
         rsqrt_of, rden_of = {}, {}
-        h_grouped_of, h_codes_of, h_scales_of, o_of = {}, {}, {}, {}
+        h_grouped_of, h_codes_of, h_scales_of, o_of, out_sb_of = {}, {}, {}, {}, {}
 
         def group_view(dram, g):
             rows = dram[g * GROUP_ROWS : (g + 1) * GROUP_ROWS, :]
             return rows.rearrange("(p j) e -> p j e", j=GROUP_TILES)
 
-        def load_group(g):
+        def load_sx(g):
             sx_sb = inputs.tile([P, GROUP_TILES, WIDTH], BF16)
             nc.sync.dma_start(out=sx_sb[:], in_=group_view(state_x, g))
+            sx_of[g] = sx_sb
+
+        def load_x(g):
             x_sb = inputs.tile([P, GROUP_TILES, WIDTH], BF16)
             nc.sync.dma_start(out=x_sb[:], in_=group_view(x, g))
+            x_of[g] = x_sb
+
+        def load_den(g):
             den_sb = inputs.tile([P, GROUP_TILES, WIDTH], BF16)
             nc.sync.dma_start(out=den_sb[:], in_=group_view(wkv_den, g))
-            num_sb = late_inputs.tile([P, GROUP_TILES, WIDTH], BF16)
+            den_of[g] = den_sb
+
+        def load_num(g):
+            num_sb = inputs.tile([P, GROUP_TILES, WIDTH], BF16)
             nc.sync.dma_start(out=num_sb[:], in_=group_view(wkv_num, g))
-            sx_of[g], x_of[g], den_of[g], num_of[g] = sx_sb, x_sb, den_sb, num_sb
+            num_of[g] = num_sb
 
         def load_weight(words, scales, label):
             codes = consts.tile([P, PACK * WIDTH], U8, name=label + "_codes", align_bytes=64)
@@ -92,6 +100,9 @@ def tile_rwkv_timemix_for_quant_pb_t_kernel(
         def half_of_words(bank, u, e):
             return bank[:, u, :].bitcast(BF16).rearrange("p (b e) -> p b e", e=HALVES)[:, :, e]
 
+        def as_halves(bank):
+            return bank[:].rearrange("p u b -> p (u b)").bitcast(BF16)
+
         def transpose_words(source, bank):
             for j in range(GROUP_TILES):
                 as_words = source[:, j, :].bitcast(F32)
@@ -102,14 +113,25 @@ def tile_rwkv_timemix_for_quant_pb_t_kernel(
                         identity[:],
                     )
 
-        def transpose_inputs(g):
+        def transpose_sx(g):
             sxw = words_psum.tile([P, WORDS, GROUP_ROWS], F32)
             transpose_words(sx_of[g], sxw)
+            sxw_of[g] = sxw
+
+        def transpose_x(g):
             xw = words_psum.tile([P, WORDS, GROUP_ROWS], F32)
             transpose_words(x_of[g], xw)
+            xw_of[g] = xw
+
+        def transpose_den(g):
             denw = words_psum.tile([P, WORDS, GROUP_ROWS], F32)
             transpose_words(den_of[g], denw)
-            sxw_of[g], xw_of[g], denw_of[g] = sxw, xw, denw
+            denw_of[g] = denw
+
+        def transpose_num(g):
+            numw = words_psum.tile([P, WORDS, GROUP_ROWS], F32)
+            transpose_words(num_of[g], numw)
+            numw_of[g] = numw
 
         def scale_state(g):
             kept = work.tile([P, PACK, GROUP_ROWS], F32)
@@ -166,102 +188,108 @@ def tile_rwkv_timemix_for_quant_pb_t_kernel(
             quantise(h_grouped_of[g], h_codes, h_scales)
             h_codes_of[g], h_scales_of[g] = h_codes, h_scales
 
-        def one_pass(acc, codes, scales, j, weight_codes, weight_plane):
-            nc.tensor.matmul_mx(
-                out=acc[:],
-                lhsT=codes[:, j * P : (j + 1) * P].bitcast(FP8X4),
-                lhsT_scale=scales[:, j * P : (j + 1) * P],
-                rhs=weight_codes[:].bitcast(FP8X4),
-                rhs_scale=weight_plane[:],
-                start=True,
-                stop=True,
-            )
-
         def receptance_matmul(g):
             for j in range(GROUP_TILES):
-                z = gate_psum.tile([P, WIDTH], F32, tag="gate")
-                one_pass(z, xr_codes_of[g], xr_scales_of[g], j, wr_codes, wr_plane)
+                z = gate_psum.tile([P, PACK, P], F32)
+                for t in range(PACK):
+                    nc.tensor.matmul_mx(
+                        out=z[:, t, :],
+                        lhsT=wr_sorted[:, t * P : (t + 1) * P].bitcast(FP8X4),
+                        lhsT_scale=wr_sorted_plane[:, t * P : (t + 1) * P],
+                        rhs=xr_codes_of[g][:, j * P : (j + 1) * P].bitcast(FP8X4),
+                        rhs_scale=xr_scales_of[g][:, j * P : (j + 1) * P],
+                        start=True,
+                        stop=True,
+                    )
                 z_of[g, j] = z
 
         def output_matmul(g):
             for j in range(GROUP_TILES):
                 o = out_psum.tile([P, WIDTH], F32)
-                one_pass(o, h_codes_of[g], h_scales_of[g], j, wo_codes, wo_plane)
+                nc.tensor.matmul_mx(
+                    out=o[:],
+                    lhsT=h_codes_of[g][:, j * P : (j + 1) * P].bitcast(FP8X4),
+                    lhsT_scale=h_scales_of[g][:, j * P : (j + 1) * P],
+                    rhs=wo_codes[:].bitcast(FP8X4),
+                    rhs_scale=wo_plane[:],
+                    start=True,
+                    stop=True,
+                )
                 o_of[g, j] = o
 
         def clip_below(g):
-            lower = work.tile([P, GROUP_TILES, WIDTH], F32)
+            lower = work.tile([P, WORDS, GROUP_ROWS, HALVES], F32)
             for j in range(GROUP_TILES):
                 nc.scalar.activation(
-                    out=lower[:, j, :], in_=z_of[g, j][:], func=ACT.Relu, scale=1.0 / 6.0, bias=half[:]
+                    out=lower[:, :, j * P : (j + 1) * P, :],
+                    in_=z_of[g, j][:].rearrange("p (u e) b -> p u b e", e=HALVES),
+                    func=ACT.Relu,
+                    scale=1.0 / 6.0,
+                    bias=half[:],
                 )
             lower_of[g] = lower
 
         def gate_num(g):
-            gated = work.tile([P, GROUP_TILES, PACK, P], F32)
-            for j in range(GROUP_TILES):
-                nc.vector.scalar_tensor_tensor(
-                    out=gated[:, j, :, :].rearrange("b t p -> b p t"),
-                    in0=lower_of[g][:, j, :].rearrange("b (p t) -> b p t", t=PACK),
-                    scalar=1.0,
-                    in1=num_of[g][:, j, :].rearrange("b (p t) -> b p t", t=PACK),
-                    op0=ALU.min,
-                    op1=ALU.mult,
-                )
+            gated = work.tile([P, WORDS, GROUP_ROWS, HALVES], F32)
+            nc.vector.scalar_tensor_tensor(
+                out=gated[:].rearrange("p u b e -> p (u b e)"),
+                in0=lower_of[g][:].rearrange("p u b e -> p (u b e)"),
+                scalar=1.0,
+                in1=as_halves(numw_of[g]),
+                op0=ALU.min,
+                op1=ALU.mult,
+            )
             gated_of[g] = gated
 
-        def transpose_gated(g):
-            for j in range(GROUP_TILES):
-                gated_t = gate_psum.tile([P, PACK, P], F32, tag="gate")
-                for t in range(PACK):
-                    nc.tensor.transpose(gated_t[:, t, :], gated_of[g][:, j, t, :], identity[:])
-                gated_t_of[g, j] = gated_t
-
         def rsqrt_den(g):
-            rsqrt = work.tile([P, GROUP_ROWS, WORDS, HALVES], F32)
-            halves = denw_of[g][:].rearrange("p u b -> p (u b)").bitcast(BF16)
-            nc.scalar.activation(
-                out=rsqrt[:],
-                in_=halves.rearrange("p (u b e) -> p b u e", u=WORDS, e=HALVES),
-                func=ACT.Abs_reciprocal_sqrt,
-            )
+            rsqrt = work.tile([P, PACK * GROUP_ROWS], F32)
+            nc.scalar.activation(out=rsqrt[:], in_=as_halves(denw_of[g]), func=ACT.Abs_reciprocal_sqrt)
             rsqrt_of[g] = rsqrt
 
         def square_rsqrt(g):
-            rden = work.tile([P, GROUP_ROWS, PACK], F32)
+            rden = work.tile([P, WORDS, GROUP_ROWS, HALVES], F32)
             nc.scalar.activation(
-                out=rden[:], in_=rsqrt_of[g][:].rearrange("p b u e -> p b (u e)"), func=ACT.Square
+                out=rden[:].rearrange("p u b e -> p (u b e)"), in_=rsqrt_of[g][:], func=ACT.Square
             )
             rden_of[g] = rden
 
         def divide(g):
             h_grouped = work.tile([P, GROUP_ROWS, PACK], BF16, align_bytes=64)
-            for j in range(GROUP_TILES):
-                nc.vector.tensor_tensor(
-                    out=h_grouped[:, j * P : (j + 1) * P, :],
-                    in0=gated_t_of[g, j][:].rearrange("p t b -> p b t"),
-                    in1=rden_of[g][:, j * P : (j + 1) * P, :],
-                    op=ALU.mult,
-                )
+            nc.gpsimd.tensor_tensor(
+                out=h_grouped[:].rearrange("p b (u e) -> p b u e", e=HALVES),
+                in0=gated_of[g][:].rearrange("p u b e -> p b u e"),
+                in1=rden_of[g][:].rearrange("p u b e -> p b u e"),
+                op=ALU.mult,
+            )
             h_grouped_of[g] = h_grouped
 
-        def store_out(g):
-            out_sb = work.tile([P, GROUP_TILES, WIDTH], F32)
-            nc.scalar.copy(out=out_sb[:, 0, :], in_=o_of[g, 0][:])
-            if g % 2 == 1:
-                nc.scalar.copy(out=out_sb[:, 1, :], in_=o_of[g, 1][:])
+        def empty_out(g, j):
+            if j == 0:
+                out_sb = work.tile([P, GROUP_TILES, WIDTH], F32)
+                out_sb_of[g] = out_sb
+            if (g, j) in SCALAR_EMPTIES:
+                nc.scalar.copy(out=out_sb_of[g][:, j, :], in_=o_of[g, j][:])
             else:
-                nc.vector.tensor_copy(out=out_sb[:, 1, :], in_=o_of[g, 1][:])
-            nc.sync.dma_start(out=group_view(out, g), in_=out_sb[:])
+                nc.vector.tensor_copy(out=out_sb_of[g][:, j, :], in_=o_of[g, j][:])
+
+        def store_out(g):
+            nc.sync.dma_start(out=group_view(out, g), in_=out_sb_of[g][:])
+
+        SCALAR_EMPTIES = ((GROUPS - 3, 1), (GROUPS - 2, 0), (GROUPS - 2, 1), (GROUPS - 1, 0))
 
         mix_bf = consts.tile([P, PACK], BF16)
         nc.sync.dma_start(out=mix_bf[:], in_=time_mix_r[0].rearrange("(p t) -> p t", t=PACK))
-        load_group(0)
+        load_sx(0)
+        load_x(0)
         wr_codes, wr_plane = load_weight(W_receptance_words, W_receptance_scales, "wr")
-        load_group(1)
+        load_den(0)
+        load_sx(1)
+        load_x(1)
+        load_num(0)
         wo_codes, wo_plane = load_weight(W_output_words, W_output_scales, "wo")
-        for g in range(2, GROUPS_AHEAD):
-            load_group(g)
+        load_den(1)
+        load_sx(2)
+        load_x(2)
 
         identity = consts.tile([P, P], F32)
         make_identity(nc, identity[:])
@@ -273,39 +301,60 @@ def tile_rwkv_timemix_for_quant_pb_t_kernel(
         nc.vector.tensor_scalar(
             out=one_minus_mix[:], in0=mix_bf[:], scalar1=-1.0, scalar2=1.0, op0=ALU.mult, op1=ALU.add
         )
+        wr_sorted = consts.tile([P, WIDTH], U32, align_bytes=64)
+        nc.vector.tensor_copy(
+            out=wr_sorted[:].bitcast(I32).rearrange("p (t m) -> p t m", t=PACK),
+            in_=wr_codes[:].bitcast(I32).rearrange("p (m t) -> p t m", t=PACK),
+        )
+        wr_sorted_plane = consts.tile([P, WIDTH], U8, align_bytes=64)
+        nc.vector.tensor_copy(
+            out=wr_sorted_plane[:].rearrange("p (t m) -> p m t", t=PACK),
+            in_=wr_plane[:].rearrange("p (m t) -> p m t", t=PACK),
+        )
 
         def live(g):
             return 0 <= g < GROUPS
 
-        for turn in range(-2, GROUPS + 3):
-            if live(turn + 1):
-                scale_state(turn + 1)
-            if live(turn - 1):
-                gate_num(turn - 1)
+        for turn in range(-2, GROUPS + 2):
             if live(turn - 2):
                 quantise_h(turn - 2)
             if live(turn):
                 quantise_xr(turn)
-            if live(turn + 1):
-                rsqrt_den(turn + 1)
-            if live(turn - 1):
-                transpose_gated(turn - 1)
-            if live(turn):
-                receptance_matmul(turn)
             if live(turn - 2):
                 output_matmul(turn - 2)
+            if live(turn):
+                receptance_matmul(turn)
+            if live(turn + 1):
+                scale_state(turn + 1)
             if live(turn - 1):
+                gate_num(turn - 1)
                 divide(turn - 1)
-            if live(turn - 3):
-                store_out(turn - 3)
+            if live(turn):
+                square_rsqrt(turn)
+            if live(turn - 2):
+                empty_out(turn - 2, 0)
+            if live(turn + 2):
+                transpose_sx(turn + 2)
+            if live(turn + 1):
+                transpose_den(turn + 1)
+            if live(turn):
+                transpose_num(turn)
+                clip_below(turn)
             if live(turn + 1):
                 mix_in_x(turn + 1)
-            if live(turn):
-                clip_below(turn)
-                square_rsqrt(turn)
+            if live(turn + 2):
+                transpose_x(turn + 2)
+            if live(turn - 2):
+                empty_out(turn - 2, 1)
             if live(turn + 1):
                 regroup_xr(turn + 1)
+                rsqrt_den(turn + 1)
             if live(turn + 2 + GROUPS_AHEAD):
-                load_group(turn + 2 + GROUPS_AHEAD)
-            if live(turn + 2):
-                transpose_inputs(turn + 2)
+                load_sx(turn + 2 + GROUPS_AHEAD)
+                load_x(turn + 2 + GROUPS_AHEAD)
+            if live(turn + 1 + GROUPS_AHEAD):
+                load_den(turn + 1 + GROUPS_AHEAD)
+            if live(turn + GROUPS_AHEAD):
+                load_num(turn + GROUPS_AHEAD)
+            if live(turn - 2):
+                store_out(turn - 2)

@@ -46,6 +46,7 @@ def tile_rwkv_timemix_for_quant_pb_t_kernel(
         consts = ctx.enter_context(tc.tile_pool(name="consts", bufs=1))
         inputs = ctx.enter_context(tc.tile_pool(name="inputs", bufs=GROUPS_AHEAD + 2))
         work = ctx.enter_context(tc.tile_pool(name="work", bufs=3))
+        handoff = ctx.enter_context(tc.tile_pool(name="handoff", bufs=1))
         words_psum = ctx.enter_context(tc.psum_pool(name="words_psum", bufs=1))
         gate_psum = ctx.enter_context(tc.psum_pool(name="gate_psum", bufs=2))
         out_psum = ctx.enter_context(tc.psum_pool(name="out_psum", bufs=2))
@@ -254,7 +255,7 @@ def tile_rwkv_timemix_for_quant_pb_t_kernel(
             rden_of[g] = rden
 
         def divide(g):
-            h_grouped = work.tile([P, GROUP_ROWS, PACK], BF16, align_bytes=64)
+            h_grouped = handoff.tile([P, GROUP_ROWS, PACK], BF16, align_bytes=64)
             nc.gpsimd.tensor_tensor(
                 out=h_grouped[:].rearrange("p b (u e) -> p b u e", e=HALVES),
                 in0=gated_of[g][:].rearrange("p u b e -> p b u e"),
@@ -315,24 +316,24 @@ def tile_rwkv_timemix_for_quant_pb_t_kernel(
         def live(g):
             return 0 <= g < GROUPS
 
-        for turn in range(-2, GROUPS + 2):
-            if live(turn - 2):
-                quantise_h(turn - 2)
+        for turn in range(-2, GROUPS + 3):
             if live(turn):
                 quantise_xr(turn)
-            if live(turn - 2):
-                output_matmul(turn - 2)
+            if live(turn - 3):
+                quantise_h(turn - 3)
+                output_matmul(turn - 3)
             if live(turn):
                 receptance_matmul(turn)
             if live(turn + 1):
                 scale_state(turn + 1)
+            if live(turn - 2):
+                divide(turn - 2)
             if live(turn - 1):
                 gate_num(turn - 1)
-                divide(turn - 1)
             if live(turn):
                 square_rsqrt(turn)
-            if live(turn - 2):
-                empty_out(turn - 2, 0)
+            if live(turn - 3):
+                empty_out(turn - 3, 0)
             if live(turn + 2):
                 transpose_sx(turn + 2)
             if live(turn + 1):
@@ -344,8 +345,8 @@ def tile_rwkv_timemix_for_quant_pb_t_kernel(
                 mix_in_x(turn + 1)
             if live(turn + 2):
                 transpose_x(turn + 2)
-            if live(turn - 2):
-                empty_out(turn - 2, 1)
+            if live(turn - 3):
+                empty_out(turn - 3, 1)
             if live(turn + 1):
                 regroup_xr(turn + 1)
                 rsqrt_den(turn + 1)
@@ -356,5 +357,5 @@ def tile_rwkv_timemix_for_quant_pb_t_kernel(
                 load_den(turn + 1 + GROUPS_AHEAD)
             if live(turn + GROUPS_AHEAD):
                 load_num(turn + GROUPS_AHEAD)
-            if live(turn - 2):
-                store_out(turn - 2)
+            if live(turn - 3):
+                store_out(turn - 3)

@@ -25,6 +25,10 @@ GROUPS_AHEAD = 3
 SCALE_ROWS = 16
 RUN = 4
 
+FIRST_VECTOR_DIVIDE = GROUPS - 2
+
+VECTOR_COLUMNS = 256
+
 FLOPS = 2 * 2 * ROWS * WIDTH * WIDTH
 
 
@@ -256,7 +260,8 @@ def tile_rwkv_timemix_for_quant_pb_t_kernel(
 
         def divide(g):
             h_grouped = handoff.tile([P, GROUP_ROWS, PACK], BF16, align_bytes=64)
-            nc.gpsimd.tensor_tensor(
+            engine = nc.vector if g >= FIRST_VECTOR_DIVIDE else nc.gpsimd
+            engine.tensor_tensor(
                 out=h_grouped[:].rearrange("p b (u e) -> p b u e", e=HALVES),
                 in0=gated_of[g][:].rearrange("p u b e -> p b u e"),
                 in1=rden_of[g][:].rearrange("p u b e -> p b u e"),
@@ -264,19 +269,32 @@ def tile_rwkv_timemix_for_quant_pb_t_kernel(
             )
             h_grouped_of[g] = h_grouped
 
+        def empty_share(g):
+            out_sb = work.tile([P, GROUP_TILES, WIDTH], F32)
+            out_sb_of[g] = out_sb
+            if (g, 1) not in SCALAR_EMPTIES:
+                nc.scalar.copy(out=out_sb[:, 1, VECTOR_COLUMNS:], in_=o_of[g, 1][:, VECTOR_COLUMNS:])
+
         def empty_out(g, j):
-            if j == 0:
-                out_sb = work.tile([P, GROUP_TILES, WIDTH], F32)
-                out_sb_of[g] = out_sb
             if (g, j) in SCALAR_EMPTIES:
                 nc.scalar.copy(out=out_sb_of[g][:, j, :], in_=o_of[g, j][:])
+            elif j == 1:
+                nc.vector.tensor_copy(
+                    out=out_sb_of[g][:, j, :VECTOR_COLUMNS], in_=o_of[g, j][:, :VECTOR_COLUMNS]
+                )
             else:
                 nc.vector.tensor_copy(out=out_sb_of[g][:, j, :], in_=o_of[g, j][:])
 
         def store_out(g):
             nc.sync.dma_start(out=group_view(out, g), in_=out_sb_of[g][:])
 
-        SCALAR_EMPTIES = ((GROUPS - 3, 1), (GROUPS - 2, 0), (GROUPS - 2, 1), (GROUPS - 1, 0))
+        SCALAR_EMPTIES = (
+            (GROUPS - 3, 0),
+            (GROUPS - 3, 1),
+            (GROUPS - 2, 0),
+            (GROUPS - 2, 1),
+            (GROUPS - 1, 0),
+        )
 
         mix_bf = consts.tile([P, PACK], BF16)
         nc.sync.dma_start(out=mix_bf[:], in_=time_mix_r[0].rearrange("(p t) -> p t", t=PACK))
@@ -317,15 +335,18 @@ def tile_rwkv_timemix_for_quant_pb_t_kernel(
             return 0 <= g < GROUPS
 
         for turn in range(-2, GROUPS + 3):
+            if live(turn - 3):
+                quantise_h(turn - 3)
             if live(turn):
                 quantise_xr(turn)
             if live(turn - 3):
-                quantise_h(turn - 3)
                 output_matmul(turn - 3)
             if live(turn):
                 receptance_matmul(turn)
             if live(turn + 1):
                 scale_state(turn + 1)
+            if live(turn - 3):
+                empty_share(turn - 3)
             if live(turn - 2):
                 divide(turn - 2)
             if live(turn - 1):

@@ -27,7 +27,7 @@ RUN = 4
 
 FIRST_VECTOR_DIVIDE = GROUPS - 2
 
-VECTOR_COLUMNS = 256
+VECTOR_COLUMNS = 384
 
 FLOPS = 2 * 2 * ROWS * WIDTH * WIDTH
 
@@ -300,15 +300,15 @@ def tile_rwkv_timemix_for_quant_pb_t_kernel(
         nc.sync.dma_start(out=mix_bf[:], in_=time_mix_r[0].rearrange("(p t) -> p t", t=PACK))
         load_sx(0)
         load_x(0)
-        wr_codes, wr_plane = load_weight(W_receptance_words, W_receptance_scales, "wr")
-        load_den(0)
         load_sx(1)
+        load_den(0)
         load_x(1)
-        load_num(0)
-        wo_codes, wo_plane = load_weight(W_output_words, W_output_scales, "wo")
-        load_den(1)
+        wr_codes, wr_plane = load_weight(W_receptance_words, W_receptance_scales, "wr")
         load_sx(2)
+        load_den(1)
+        load_num(0)
         load_x(2)
+        wo_codes, wo_plane = load_weight(W_output_words, W_output_scales, "wo")
 
         identity = consts.tile([P, P], F32)
         make_identity(nc, identity[:])
@@ -321,15 +321,21 @@ def tile_rwkv_timemix_for_quant_pb_t_kernel(
             out=one_minus_mix[:], in0=mix_bf[:], scalar1=-1.0, scalar2=1.0, op0=ALU.mult, op1=ALU.add
         )
         wr_sorted = consts.tile([P, WIDTH], U32, align_bytes=64)
-        nc.vector.tensor_copy(
-            out=wr_sorted[:].bitcast(I32).rearrange("p (t m) -> p t m", t=PACK),
-            in_=wr_codes[:].bitcast(I32).rearrange("p (m t) -> p t m", t=PACK),
-        )
         wr_sorted_plane = consts.tile([P, WIDTH], U8, align_bytes=64)
-        nc.vector.tensor_copy(
-            out=wr_sorted_plane[:].rearrange("p (t m) -> p m t", t=PACK),
-            in_=wr_plane[:].rearrange("p (m t) -> p m t", t=PACK),
-        )
+
+        def sort_receptance():
+            nc.vector.tensor_copy(
+                out=wr_sorted[:].bitcast(I32).rearrange("p (t m) -> p t m", t=PACK),
+                in_=wr_codes[:].bitcast(I32).rearrange("p (m t) -> p t m", t=PACK),
+            )
+            nc.vector.tensor_copy(
+                out=wr_sorted_plane[:].rearrange("p (t m) -> p m t", t=PACK),
+                in_=wr_plane[:].rearrange("p (m t) -> p m t", t=PACK),
+            )
+
+        warm = consts.tile([P, 1], F32)
+        for func in (ACT.Relu, ACT.Square, ACT.Copy, ACT.Abs_reciprocal_sqrt):
+            nc.scalar.activation(out=warm[:], in_=half[:], func=func)
 
         def live(g):
             return 0 <= g < GROUPS
@@ -371,6 +377,8 @@ def tile_rwkv_timemix_for_quant_pb_t_kernel(
             if live(turn + 1):
                 regroup_xr(turn + 1)
                 rsqrt_den(turn + 1)
+            if turn == -1:
+                sort_receptance()
             if live(turn + 2 + GROUPS_AHEAD):
                 load_sx(turn + 2 + GROUPS_AHEAD)
                 load_x(turn + 2 + GROUPS_AHEAD)

@@ -27,7 +27,7 @@ RUN = 4
 
 FIRST_VECTOR_DIVIDE = GROUPS - 2
 
-VECTOR_COLUMNS = 384
+VECTOR_COLUMNS = 512
 
 FLOPS = 2 * 2 * ROWS * WIDTH * WIDTH
 
@@ -272,7 +272,7 @@ def tile_rwkv_timemix_for_quant_pb_t_kernel(
         def empty_share(g):
             out_sb = work.tile([P, GROUP_TILES, WIDTH], F32)
             out_sb_of[g] = out_sb
-            if (g, 1) not in SCALAR_EMPTIES:
+            if (g, 1) not in SCALAR_EMPTIES and VECTOR_COLUMNS < WIDTH:
                 nc.scalar.copy(out=out_sb[:, 1, VECTOR_COLUMNS:], in_=o_of[g, 1][:, VECTOR_COLUMNS:])
 
         def empty_out(g, j):

@@ -23,7 +23,7 @@ GROUP_ROWS = GROUP_TILES * P
 GROUPS = ROWS // GROUP_ROWS
 GROUPS_AHEAD = 3
 SCALE_ROWS = 16
-RUN = 4
+RUN = 8
 
 FIRST_VECTOR_DIVIDE = GROUPS - 2
 

@@ -14,6 +14,7 @@ ALU = mybir.AluOpType
 
 P = 128
 PACK = 4
+ALL_ROWS = slice(0, 256)
 HALVES = 2
 WORDS = PACK // HALVES
 ROWS = 4096
@@ -24,10 +25,6 @@ GROUPS = ROWS // GROUP_ROWS
 GROUPS_AHEAD = 3
 SCALE_ROWS = 16
 RUN = 8
-
-FIRST_VECTOR_DIVIDE = GROUPS - 2
-
-VECTOR_COLUMNS = 512
 
 FLOPS = 2 * 2 * ROWS * WIDTH * WIDTH
 
@@ -174,24 +171,25 @@ def tile_rwkv_timemix_for_quant_pb_t_kernel(
             )
             xr_grouped_of[g] = xr_grouped
 
-        def quantise(grouped, codes, scales):
+        def quantise(grouped, codes, scales, rows):
             nc.vector.quantize_mx(
-                out=codes[:].bitcast(FP8X4),
-                scales=scales[:],
-                in_=grouped[:].rearrange("p b t -> p (b t)"),
+                out=codes[:, rows].bitcast(FP8X4),
+                scales=scales[:, rows],
+                in_=grouped[:, rows, :].rearrange("p b t -> p (b t)"),
             )
 
         def quantise_xr(g):
             xr_codes = work.tile([P, GROUP_ROWS], U32, align_bytes=64)
             xr_scales = work.tile([P, GROUP_ROWS], U8, align_bytes=64)
-            quantise(xr_grouped_of[g], xr_codes, xr_scales)
+            quantise(xr_grouped_of[g], xr_codes, xr_scales, ALL_ROWS)
             xr_codes_of[g], xr_scales_of[g] = xr_codes, xr_scales
 
-        def quantise_h(g):
-            h_codes = work.tile([P, GROUP_ROWS], U32, align_bytes=64)
-            h_scales = work.tile([P, GROUP_ROWS], U8, align_bytes=64)
-            quantise(h_grouped_of[g], h_codes, h_scales)
-            h_codes_of[g], h_scales_of[g] = h_codes, h_scales
+        def quantise_h(g, rows=ALL_ROWS):
+            if g not in h_codes_of:
+                h_codes = work.tile([P, GROUP_ROWS], U32, align_bytes=64)
+                h_scales = work.tile([P, GROUP_ROWS], U8, align_bytes=64)
+                h_codes_of[g], h_scales_of[g] = h_codes, h_scales
+            quantise(h_grouped_of[g], h_codes_of[g], h_scales_of[g], rows)
 
         def receptance_matmul(g):
             for j in range(GROUP_TILES):
@@ -208,19 +206,18 @@ def tile_rwkv_timemix_for_quant_pb_t_kernel(
                     )
                 z_of[g, j] = z
 
-        def output_matmul(g):
-            for j in range(GROUP_TILES):
-                o = out_psum.tile([P, WIDTH], F32)
-                nc.tensor.matmul_mx(
-                    out=o[:],
-                    lhsT=h_codes_of[g][:, j * P : (j + 1) * P].bitcast(FP8X4),
-                    lhsT_scale=h_scales_of[g][:, j * P : (j + 1) * P],
-                    rhs=wo_codes[:].bitcast(FP8X4),
-                    rhs_scale=wo_plane[:],
-                    start=True,
-                    stop=True,
-                )
-                o_of[g, j] = o
+        def output_matmul(g, j):
+            o = out_psum.tile([P, WIDTH], F32)
+            nc.tensor.matmul_mx(
+                out=o[:],
+                lhsT=h_codes_of[g][:, j * P : (j + 1) * P].bitcast(FP8X4),
+                lhsT_scale=h_scales_of[g][:, j * P : (j + 1) * P],
+                rhs=wo_codes[:].bitcast(FP8X4),
+                rhs_scale=wo_plane[:],
+                start=True,
+                stop=True,
+            )
+            o_of[g, j] = o
 
         def clip_below(g):
             lower = work.tile([P, WORDS, GROUP_ROWS, HALVES], F32)
@@ -234,17 +231,19 @@ def tile_rwkv_timemix_for_quant_pb_t_kernel(
                 )
             lower_of[g] = lower
 
-        def gate_num(g):
-            gated = work.tile([P, WORDS, GROUP_ROWS, HALVES], F32)
+        def gate_num(g, rows=ALL_ROWS):
+            if g not in gated_of:
+                gated = work.tile([P, WORDS, GROUP_ROWS, HALVES], F32)
+                gated_of[g] = gated
+            num_rows = as_halves(numw_of[g]).rearrange("p (u b e) -> p u b e", u=WORDS, e=HALVES)[:, :, rows, :]
             nc.vector.scalar_tensor_tensor(
-                out=gated[:].rearrange("p u b e -> p (u b e)"),
-                in0=lower_of[g][:].rearrange("p u b e -> p (u b e)"),
+                out=gated_of[g][:, :, rows, :].rearrange("p u b e -> p u (b e)"),
+                in0=lower_of[g][:, :, rows, :].rearrange("p u b e -> p u (b e)"),
                 scalar=1.0,
-                in1=as_halves(numw_of[g]),
+                in1=num_rows.rearrange("p u b e -> p u (b e)"),
                 op0=ALU.min,
                 op1=ALU.mult,
             )
-            gated_of[g] = gated
 
         def rsqrt_den(g):
             rsqrt = work.tile([P, PACK * GROUP_ROWS], F32)
@@ -258,35 +257,31 @@ def tile_rwkv_timemix_for_quant_pb_t_kernel(
             )
             rden_of[g] = rden
 
-        def divide(g):
-            h_grouped = handoff.tile([P, GROUP_ROWS, PACK], BF16, align_bytes=64)
-            engine = nc.vector if g >= FIRST_VECTOR_DIVIDE else nc.gpsimd
+        def divide(g, engine, rows=ALL_ROWS):
+            if g not in h_grouped_of:
+                h_grouped = handoff.tile([P, GROUP_ROWS, PACK], BF16, align_bytes=64)
+                h_grouped_of[g] = h_grouped
             engine.tensor_tensor(
-                out=h_grouped[:].rearrange("p b (u e) -> p b u e", e=HALVES),
-                in0=gated_of[g][:].rearrange("p u b e -> p b u e"),
-                in1=rden_of[g][:].rearrange("p u b e -> p b u e"),
+                out=h_grouped_of[g][:, rows, :].rearrange("p b (u e) -> p b u e", e=HALVES),
+                in0=gated_of[g][:, :, rows, :].rearrange("p u b e -> p b u e"),
+                in1=rden_of[g][:, :, rows, :].rearrange("p u b e -> p b u e"),
                 op=ALU.mult,
             )
-            h_grouped_of[g] = h_grouped
-
-        def empty_share(g):
-            out_sb = work.tile([P, GROUP_TILES, WIDTH], F32)
-            out_sb_of[g] = out_sb
-            if (g, 1) not in SCALAR_EMPTIES and VECTOR_COLUMNS < WIDTH:
-                nc.scalar.copy(out=out_sb[:, 1, VECTOR_COLUMNS:], in_=o_of[g, 1][:, VECTOR_COLUMNS:])
 
         def empty_out(g, j):
+            if j == 0:
+                out_sb = work.tile([P, GROUP_TILES, WIDTH], F32)
+                out_sb_of[g] = out_sb
             if (g, j) in SCALAR_EMPTIES:
                 nc.scalar.copy(out=out_sb_of[g][:, j, :], in_=o_of[g, j][:])
-            elif j == 1:
-                nc.vector.tensor_copy(
-                    out=out_sb_of[g][:, j, :VECTOR_COLUMNS], in_=o_of[g, j][:, :VECTOR_COLUMNS]
-                )
             else:
                 nc.vector.tensor_copy(out=out_sb_of[g][:, j, :], in_=o_of[g, j][:])
 
         def store_out(g):
             nc.sync.dma_start(out=group_view(out, g), in_=out_sb_of[g][:])
+
+        def store_tile(g, j):
+            nc.sync.dma_start(out=group_view(out, g)[:, j, :], in_=out_sb_of[g][:, j, :])
 
         SCALAR_EMPTIES = (
             (GROUPS - 3, 0),
@@ -334,37 +329,36 @@ def tile_rwkv_timemix_for_quant_pb_t_kernel(
             )
 
         warm = consts.tile([P, 1], F32)
-        for func in (ACT.Relu, ACT.Square, ACT.Copy, ACT.Abs_reciprocal_sqrt):
+        for func in (ACT.Abs_reciprocal_sqrt, ACT.Relu, ACT.Square, ACT.Copy):
             nc.scalar.activation(out=warm[:], in_=half[:], func=func)
 
         def live(g):
             return 0 <= g < GROUPS
 
-        for turn in range(-2, GROUPS + 3):
+        for turn in range(-2, GROUPS):
             if live(turn - 3):
                 quantise_h(turn - 3)
             if live(turn):
                 quantise_xr(turn)
             if live(turn - 3):
-                output_matmul(turn - 3)
+                output_matmul(turn - 3, 0)
+                output_matmul(turn - 3, 1)
             if live(turn):
                 receptance_matmul(turn)
             if live(turn + 1):
                 scale_state(turn + 1)
-            if live(turn - 3):
-                empty_share(turn - 3)
             if live(turn - 2):
-                divide(turn - 2)
+                divide(turn - 2, nc.gpsimd)
             if live(turn - 1):
                 gate_num(turn - 1)
             if live(turn):
                 square_rsqrt(turn)
             if live(turn - 3):
                 empty_out(turn - 3, 0)
-            if live(turn + 2):
-                transpose_sx(turn + 2)
             if live(turn + 1):
                 transpose_den(turn + 1)
+            if live(turn + 2):
+                transpose_sx(turn + 2)
             if live(turn):
                 transpose_num(turn)
                 clip_below(turn)
@@ -388,3 +382,31 @@ def tile_rwkv_timemix_for_quant_pb_t_kernel(
                 load_num(turn + GROUPS_AHEAD)
             if live(turn - 3):
                 store_out(turn - 3)
+
+        last = GROUPS - 1
+        tile_rows = [slice(j * P, (j + 1) * P) for j in range(GROUP_TILES)]
+
+        def finish(g):
+            for j in range(GROUP_TILES):
+                output_matmul(g, j)
+                empty_out(g, j)
+            store_out(g)
+
+        quantise_h(last - 2)
+        divide(last - 1, nc.vector, tile_rows[0])
+        divide(last - 1, nc.gpsimd, tile_rows[1])
+        gate_num(last, tile_rows[0])
+        finish(last - 2)
+        quantise_h(last - 1)
+        divide(last, nc.vector, tile_rows[0])
+        gate_num(last, tile_rows[1])
+        finish(last - 1)
+        quantise_h(last, tile_rows[0])
+        divide(last, nc.vector, tile_rows[1])
+        output_matmul(last, 0)
+        empty_out(last, 0)
+        store_tile(last, 0)
+        quantise_h(last, tile_rows[1])
+        output_matmul(last, 1)
+        empty_out(last, 1)
+        store_tile(last, 1)

@@ -26,6 +26,9 @@ GROUPS_AHEAD = 3
 SCALE_ROWS = 16
 RUN = 8
 
+SCALAR_SQUARES = 896
+VECTOR_COLUMNS = 416
+
 FLOPS = 2 * 2 * ROWS * WIDTH * WIDTH
 
 
@@ -227,7 +230,7 @@ def tile_rwkv_timemix_for_quant_pb_t_kernel(
                     in_=z_of[g, j][:].rearrange("p (u e) b -> p u b e", e=HALVES),
                     func=ACT.Relu,
                     scale=1.0 / 6.0,
-                    bias=half[:],
+                    bias=0.5,
                 )
             lower_of[g] = lower
 
@@ -252,10 +255,21 @@ def tile_rwkv_timemix_for_quant_pb_t_kernel(
 
         def square_rsqrt(g):
             rden = work.tile([P, WORDS, GROUP_ROWS, HALVES], F32)
-            nc.scalar.activation(
-                out=rden[:].rearrange("p u b e -> p (u b e)"), in_=rsqrt_of[g][:], func=ACT.Square
-            )
             rden_of[g] = rden
+            nc.scalar.activation(
+                out=rden[:].rearrange("p u b e -> p (u b e)")[:, :SCALAR_SQUARES],
+                in_=rsqrt_of[g][:, :SCALAR_SQUARES],
+                func=ACT.Square,
+            )
+
+        def square_rest(g):
+            rest = rsqrt_of[g][:, SCALAR_SQUARES:]
+            nc.gpsimd.tensor_tensor(
+                out=rden_of[g][:].rearrange("p u b e -> p (u b e)")[:, SCALAR_SQUARES:],
+                in0=rest,
+                in1=rest,
+                op=ALU.mult,
+            )
 
         def divide(g, engine, rows=ALL_ROWS):
             if g not in h_grouped_of:
@@ -268,28 +282,23 @@ def tile_rwkv_timemix_for_quant_pb_t_kernel(
                 op=ALU.mult,
             )
 
-        def empty_out(g, j):
-            if j == 0:
+        def empty_share(g):
+            out_sb = work.tile([P, GROUP_TILES, WIDTH], F32)
+            out_sb_of[g] = out_sb
+            nc.scalar.copy(out=out_sb[:, 1, VECTOR_COLUMNS:], in_=o_of[g, 1][:, VECTOR_COLUMNS:])
+
+        def empty_out(g, j, engine, columns=slice(0, WIDTH)):
+            if g not in out_sb_of:
                 out_sb = work.tile([P, GROUP_TILES, WIDTH], F32)
                 out_sb_of[g] = out_sb
-            if (g, j) in SCALAR_EMPTIES:
-                nc.scalar.copy(out=out_sb_of[g][:, j, :], in_=o_of[g, j][:])
-            else:
-                nc.vector.tensor_copy(out=out_sb_of[g][:, j, :], in_=o_of[g, j][:])
+            copy = nc.scalar.copy if engine is nc.scalar else nc.vector.tensor_copy
+            copy(out=out_sb_of[g][:, j, columns], in_=o_of[g, j][:, columns])
 
         def store_out(g):
             nc.sync.dma_start(out=group_view(out, g), in_=out_sb_of[g][:])
 
         def store_tile(g, j):
             nc.sync.dma_start(out=group_view(out, g)[:, j, :], in_=out_sb_of[g][:, j, :])
-
-        SCALAR_EMPTIES = (
-            (GROUPS - 3, 0),
-            (GROUPS - 3, 1),
-            (GROUPS - 2, 0),
-            (GROUPS - 2, 1),
-            (GROUPS - 1, 0),
-        )
 
         mix_bf = consts.tile([P, PACK], BF16)
         nc.sync.dma_start(out=mix_bf[:], in_=time_mix_r[0].rearrange("(p t) -> p t", t=PACK))
@@ -347,14 +356,17 @@ def tile_rwkv_timemix_for_quant_pb_t_kernel(
                 receptance_matmul(turn)
             if live(turn + 1):
                 scale_state(turn + 1)
+            if live(turn - 3):
+                empty_share(turn - 3)
             if live(turn - 2):
                 divide(turn - 2, nc.gpsimd)
             if live(turn - 1):
                 gate_num(turn - 1)
             if live(turn):
                 square_rsqrt(turn)
+                square_rest(turn)
             if live(turn - 3):
-                empty_out(turn - 3, 0)
+                empty_out(turn - 3, 0, nc.vector)
             if live(turn + 1):
                 transpose_den(turn + 1)
             if live(turn + 2):
@@ -367,7 +379,7 @@ def tile_rwkv_timemix_for_quant_pb_t_kernel(
             if live(turn + 2):
                 transpose_x(turn + 2)
             if live(turn - 3):
-                empty_out(turn - 3, 1)
+                empty_out(turn - 3, 1, nc.vector, slice(0, VECTOR_COLUMNS))
             if live(turn + 1):
                 regroup_xr(turn + 1)
                 rsqrt_den(turn + 1)
@@ -389,7 +401,7 @@ def tile_rwkv_timemix_for_quant_pb_t_kernel(
         def finish(g):
             for j in range(GROUP_TILES):
                 output_matmul(g, j)
-                empty_out(g, j)
+                empty_out(g, j, nc.scalar)
             store_out(g)
 
         quantise_h(last - 2)
@@ -404,9 +416,9 @@ def tile_rwkv_timemix_for_quant_pb_t_kernel(
         quantise_h(last, tile_rows[0])
         divide(last, nc.vector, tile_rows[1])
         output_matmul(last, 0)
-        empty_out(last, 0)
+        empty_out(last, 0, nc.scalar)
         store_tile(last, 0)
         quantise_h(last, tile_rows[1])
         output_matmul(last, 1)
-        empty_out(last, 1)
+        empty_out(last, 1, nc.vector)
         store_tile(last, 1)

@@ -195,19 +195,20 @@ def tile_rwkv_timemix_for_quant_pb_t_kernel(
             quantise(h_grouped_of[g], h_codes_of[g], h_scales_of[g], rows)
 
         def receptance_matmul(g):
-            for j in range(GROUP_TILES):
-                z = gate_psum.tile([P, PACK, P], F32)
-                for t in range(PACK):
+            for u in range(WORDS):
+                z = gate_psum.tile([P, HALVES, GROUP_ROWS], F32)
+                for e in range(HALVES):
+                    first = (HALVES * u + e) * P
                     nc.tensor.matmul_mx(
-                        out=z[:, t, :],
-                        lhsT=wr_sorted[:, t * P : (t + 1) * P].bitcast(FP8X4),
-                        lhsT_scale=wr_sorted_plane[:, t * P : (t + 1) * P],
-                        rhs=xr_codes_of[g][:, j * P : (j + 1) * P].bitcast(FP8X4),
-                        rhs_scale=xr_scales_of[g][:, j * P : (j + 1) * P],
+                        out=z[:, e, :],
+                        lhsT=wr_sorted[:, first : first + P].bitcast(FP8X4),
+                        lhsT_scale=wr_sorted_plane[:, first : first + P],
+                        rhs=xr_codes_of[g][:].bitcast(FP8X4),
+                        rhs_scale=xr_scales_of[g][:],
                         start=True,
                         stop=True,
                     )
-                z_of[g, j] = z
+                z_of[g, u] = z
 
         def output_matmul(g, j):
             o = out_psum.tile([P, WIDTH], F32)
@@ -224,10 +225,10 @@ def tile_rwkv_timemix_for_quant_pb_t_kernel(
 
         def clip_below(g):
             lower = work.tile([P, WORDS, GROUP_ROWS, HALVES], F32)
-            for j in range(GROUP_TILES):
+            for u in range(WORDS):
                 nc.scalar.activation(
-                    out=lower[:, :, j * P : (j + 1) * P, :],
-                    in_=z_of[g, j][:].rearrange("p (u e) b -> p u b e", e=HALVES),
+                    out=lower[:, u, :, :],
+                    in_=z_of[g, u][:].rearrange("p e b -> p b e"),
                     func=ACT.Relu,
                     scale=1.0 / 6.0,
                     bias=0.5,
@@ -301,8 +302,8 @@ def tile_rwkv_timemix_for_quant_pb_t_kernel(
             nc.sync.dma_start(out=group_view(out, g)[:, j, :], in_=out_sb_of[g][:, j, :])
 
         mix_bf = consts.tile([P, PACK], BF16)
-        nc.sync.dma_start(out=mix_bf[:], in_=time_mix_r[0].rearrange("(p t) -> p t", t=PACK))
         load_sx(0)
+        nc.sync.dma_start(out=mix_bf[:], in_=time_mix_r[0].rearrange("(p t) -> p t", t=PACK))
         load_x(0)
         load_sx(1)
         load_den(0)
@@ -312,7 +313,6 @@ def tile_rwkv_timemix_for_quant_pb_t_kernel(
         load_den(1)
         load_num(0)
         load_x(2)
-        wo_codes, wo_plane = load_weight(W_output_words, W_output_scales, "wo")
 
         identity = consts.tile([P, P], F32)
         make_identity(nc, identity[:])
@@ -392,6 +392,8 @@ def tile_rwkv_timemix_for_quant_pb_t_kernel(
                 load_den(turn + 1 + GROUPS_AHEAD)
             if live(turn + GROUPS_AHEAD):
                 load_num(turn + GROUPS_AHEAD)
+            if turn == -1:
+                wo_codes, wo_plane = load_weight(W_output_words, W_output_scales, "wo")
             if live(turn - 3):
                 store_out(turn - 3)
 
@@ -419,6 +421,20 @@ def tile_rwkv_timemix_for_quant_pb_t_kernel(
         empty_out(last, 0, nc.scalar)
         store_tile(last, 0)
         quantise_h(last, tile_rows[1])
-        output_matmul(last, 1)
-        empty_out(last, 1, nc.vector)
+        last_rows = slice(P, GROUP_ROWS)
+        spare = gate_psum.tile([P, HALVES, GROUP_ROWS], F32, name="z")
+        right = out_psum.tile([P, WIDTH], F32, name="o")
+        for c, bank in enumerate((spare[:].rearrange("p e b -> p (e b)"), right[:])):
+            columns = slice(c * WIDTH // 2, (c + 1) * WIDTH // 2)
+            nc.tensor.matmul_mx(
+                out=bank[:, : WIDTH // 2],
+                lhsT=h_codes_of[last][:, last_rows].bitcast(FP8X4),
+                lhsT_scale=h_scales_of[last][:, last_rows],
+                rhs=wo_codes[:, c * PACK * WIDTH // 2 : (c + 1) * PACK * WIDTH // 2].bitcast(FP8X4),
+                rhs_scale=wo_plane[:, columns],
+                start=True,
+                stop=True,
+            )
+            copy = nc.scalar.copy if c == 0 else nc.vector.tensor_copy
+            copy(out=out_sb_of[last][:, 1, columns], in_=bank[:, : WIDTH // 2])
         store_tile(last, 1)

from contextlib import ExitStack

import concourse.mybir as mybir
from concourse.masks import make_identity

F32 = mybir.dt.float32
BF16 = mybir.dt.bfloat16
I32 = mybir.dt.int32
U8 = mybir.dt.uint8
U32 = mybir.dt.uint32
FP8X4 = mybir.dt.float8_e4m3fn_x4
ACT = mybir.ActivationFunctionType
ALU = mybir.AluOpType

P = 128
PACK = 4
ALL_ROWS = slice(0, 256)
HALVES = 2
WORDS = PACK // HALVES
ROWS = 4096
WIDTH = 512
GROUP_TILES = 2
GROUP_ROWS = GROUP_TILES * P
GROUPS = ROWS // GROUP_ROWS
GROUPS_AHEAD = 3
SCALE_ROWS = 16
RUN = 8

SCALAR_SQUARES = 896
VECTOR_COLUMNS = 416

FLOPS = 2 * 2 * ROWS * WIDTH * WIDTH


def tile_rwkv_timemix_for_quant_pb_t_kernel(
    tc,
    x,
    state_x,
    time_mix_r,
    W_receptance_words,
    W_receptance_scales,
    wkv_num,
    wkv_den,
    W_output_words,
    W_output_scales,
    out,
):
    nc = tc.nc
    with ExitStack() as ctx:
        consts = ctx.enter_context(tc.tile_pool(name="consts", bufs=1))
        inputs = ctx.enter_context(tc.tile_pool(name="inputs", bufs=GROUPS_AHEAD + 2))
        work = ctx.enter_context(tc.tile_pool(name="work", bufs=3))
        handoff = ctx.enter_context(tc.tile_pool(name="handoff", bufs=1))
        words_psum = ctx.enter_context(tc.psum_pool(name="words_psum", bufs=1))
        gate_psum = ctx.enter_context(tc.psum_pool(name="gate_psum", bufs=2))
        out_psum = ctx.enter_context(tc.psum_pool(name="out_psum", bufs=2))
        ctx.enter_context(tc.manual_schedule())

        sx_of, x_of, den_of, num_of = {}, {}, {}, {}
        sxw_of, xw_of, denw_of, numw_of = {}, {}, {}, {}
        kept_of, xr_planes_of, xr_grouped_of, xr_codes_of, xr_scales_of = {}, {}, {}, {}, {}
        z_of, lower_of, gated_of = {}, {}, {}
        rsqrt_of, rden_of = {}, {}
        h_grouped_of, h_codes_of, h_scales_of, o_of, out_sb_of = {}, {}, {}, {}, {}

        def group_view(dram, g):
            rows = dram[g * GROUP_ROWS : (g + 1) * GROUP_ROWS, :]
            return rows.rearrange("(p j) e -> p j e", j=GROUP_TILES)

        def load_sx(g):
            sx_sb = inputs.tile([P, GROUP_TILES, WIDTH], BF16)
            nc.sync.dma_start(out=sx_sb[:], in_=group_view(state_x, g))
            sx_of[g] = sx_sb

        def load_x(g):
            x_sb = inputs.tile([P, GROUP_TILES, WIDTH], BF16)
            nc.sync.dma_start(out=x_sb[:], in_=group_view(x, g))
            x_of[g] = x_sb

        def load_den(g):
            den_sb = inputs.tile([P, GROUP_TILES, WIDTH], BF16)
            nc.sync.dma_start(out=den_sb[:], in_=group_view(wkv_den, g))
            den_of[g] = den_sb

        def load_num(g):
            num_sb = inputs.tile([P, GROUP_TILES, WIDTH], BF16)
            nc.sync.dma_start(out=num_sb[:], in_=group_view(wkv_num, g))
            num_of[g] = num_sb

        def load_weight(words, scales, label):
            codes = consts.tile([P, PACK * WIDTH], U8, name=label + "_codes", align_bytes=64)
            nc.sync.dma_start(
                out=codes[:].bitcast(I32),
                in_=words[0].rearrange("p n t -> p (n t)").bitcast(I32),
            )
            plane = consts.tile([P, WIDTH], U8, name=label + "_plane", align_bytes=64)
            nc.vector.memset(plane[:].bitcast(I32), 0)
            for quadrant in range(SCALE_ROWS // PACK):
                nc.sync.dma_start(
                    out=plane[32 * quadrant : 32 * quadrant + PACK, :].bitcast(I32),
                    in_=scales[0, PACK * quadrant : PACK * (quadrant + 1), :].bitcast(I32),
                )
            return codes, plane

        def half_of_words(bank, u, e):
            return bank[:, u, :].bitcast(BF16).rearrange("p (b e) -> p b e", e=HALVES)[:, :, e]

        def as_halves(bank):
            return bank[:].rearrange("p u b -> p (u b)").bitcast(BF16)

        def transpose_words(source, bank):
            for j in range(GROUP_TILES):
                as_words = source[:, j, :].bitcast(F32)
                for u in range(WORDS):
                    nc.tensor.transpose(
                        bank[:, u, j * P : (j + 1) * P],
                        as_words[:, u : WIDTH // HALVES : WORDS],
                        identity[:],
                    )

        def transpose_sx(g):
            sxw = words_psum.tile([P, WORDS, GROUP_ROWS], F32)
            transpose_words(sx_of[g], sxw)
            sxw_of[g] = sxw

        def transpose_x(g):
            xw = words_psum.tile([P, WORDS, GROUP_ROWS], F32)
            transpose_words(x_of[g], xw)
            xw_of[g] = xw

        def transpose_den(g):
            denw = words_psum.tile([P, WORDS, GROUP_ROWS], F32)
            transpose_words(den_of[g], denw)
            denw_of[g] = denw

        def transpose_num(g):
            numw = words_psum.tile([P, WORDS, GROUP_ROWS], F32)
            transpose_words(num_of[g], numw)
            numw_of[g] = numw

        def scale_state(g):
            kept = work.tile([P, PACK, GROUP_ROWS], F32)
            for u in range(WORDS):
                for e in range(HALVES):
                    t = HALVES * u + e
                    nc.scalar.activation(
                        out=kept[:, t, :],
                        in_=half_of_words(sxw_of[g], u, e),
                        func=ACT.Copy,
                        scale=one_minus_mix[:, t : t + 1],
                    )
            kept_of[g] = kept

        def mix_in_x(g):
            xr_planes = work.tile([P, PACK, GROUP_ROWS], BF16)
            for u in range(WORDS):
                for e in range(HALVES):
                    t = HALVES * u + e
                    nc.vector.scalar_tensor_tensor(
                        out=xr_planes[:, t, :],
                        in0=half_of_words(xw_of[g], u, e),
                        scalar=mix_r[:, t : t + 1],
                        in1=kept_of[g][:, t, :],
                        op0=ALU.mult,
                        op1=ALU.add,
                    )
            xr_planes_of[g] = xr_planes

        def regroup_xr(g):
            xr_grouped = work.tile([P, GROUP_ROWS, PACK], BF16, align_bytes=64)
            nc.vector.tensor_copy(
                out=xr_grouped[:].rearrange("p (c i) t -> p c t i", i=RUN),
                in_=xr_planes_of[g][:].rearrange("p t (c i) -> p c t i", i=RUN),
            )
            xr_grouped_of[g] = xr_grouped

        def quantise(grouped, codes, scales, rows):
            nc.vector.quantize_mx(
                out=codes[:, rows].bitcast(FP8X4),
                scales=scales[:, rows],
                in_=grouped[:, rows, :].rearrange("p b t -> p (b t)"),
            )

        def quantise_xr(g):
            xr_codes = work.tile([P, GROUP_ROWS], U32, align_bytes=64)
            xr_scales = work.tile([P, GROUP_ROWS], U8, align_bytes=64)
            quantise(xr_grouped_of[g], xr_codes, xr_scales, ALL_ROWS)
            xr_codes_of[g], xr_scales_of[g] = xr_codes, xr_scales

        def quantise_h(g, rows=ALL_ROWS):
            if g not in h_codes_of:
                h_codes = work.tile([P, GROUP_ROWS], U32, align_bytes=64)
                h_scales = work.tile([P, GROUP_ROWS], U8, align_bytes=64)
                h_codes_of[g], h_scales_of[g] = h_codes, h_scales
            quantise(h_grouped_of[g], h_codes_of[g], h_scales_of[g], rows)

        def receptance_matmul(g):
            for u in range(WORDS):
                z = gate_psum.tile([P, HALVES, GROUP_ROWS], F32)
                for e in range(HALVES):
                    first = (HALVES * u + e) * P
                    nc.tensor.matmul_mx(
                        out=z[:, e, :],
                        lhsT=wr_sorted[:, first : first + P].bitcast(FP8X4),
                        lhsT_scale=wr_sorted_plane[:, first : first + P],
                        rhs=xr_codes_of[g][:].bitcast(FP8X4),
                        rhs_scale=xr_scales_of[g][:],
                        start=True,
                        stop=True,
                    )
                z_of[g, u] = z

        def output_matmul(g, j):
            o = out_psum.tile([P, WIDTH], F32)
            nc.tensor.matmul_mx(
                out=o[:],
                lhsT=h_codes_of[g][:, j * P : (j + 1) * P].bitcast(FP8X4),
                lhsT_scale=h_scales_of[g][:, j * P : (j + 1) * P],
                rhs=wo_codes[:].bitcast(FP8X4),
                rhs_scale=wo_plane[:],
                start=True,
                stop=True,
            )
            o_of[g, j] = o

        def clip_below(g):
            lower = work.tile([P, WORDS, GROUP_ROWS, HALVES], F32)
            for u in range(WORDS):
                nc.scalar.activation(
                    out=lower[:, u, :, :],
                    in_=z_of[g, u][:].rearrange("p e b -> p b e"),
                    func=ACT.Relu,
                    scale=1.0 / 6.0,
                    bias=0.5,
                )
            lower_of[g] = lower

        def gate_num(g, rows=ALL_ROWS):
            if g not in gated_of:
                gated = work.tile([P, WORDS, GROUP_ROWS, HALVES], F32)
                gated_of[g] = gated
            num_rows = as_halves(numw_of[g]).rearrange("p (u b e) -> p u b e", u=WORDS, e=HALVES)[:, :, rows, :]
            nc.vector.scalar_tensor_tensor(
                out=gated_of[g][:, :, rows, :].rearrange("p u b e -> p u (b e)"),
                in0=lower_of[g][:, :, rows, :].rearrange("p u b e -> p u (b e)"),
                scalar=1.0,
                in1=num_rows.rearrange("p u b e -> p u (b e)"),
                op0=ALU.min,
                op1=ALU.mult,
            )

        def rsqrt_den(g):
            rsqrt = work.tile([P, PACK * GROUP_ROWS], F32)
            nc.scalar.activation(out=rsqrt[:], in_=as_halves(denw_of[g]), func=ACT.Abs_reciprocal_sqrt)
            rsqrt_of[g] = rsqrt

        def square_rsqrt(g):
            rden = work.tile([P, WORDS, GROUP_ROWS, HALVES], F32)
            rden_of[g] = rden
            nc.scalar.activation(
                out=rden[:].rearrange("p u b e -> p (u b e)")[:, :SCALAR_SQUARES],
                in_=rsqrt_of[g][:, :SCALAR_SQUARES],
                func=ACT.Square,
            )

        def square_rest(g):
            rest = rsqrt_of[g][:, SCALAR_SQUARES:]
            nc.gpsimd.tensor_tensor(
                out=rden_of[g][:].rearrange("p u b e -> p (u b e)")[:, SCALAR_SQUARES:],
                in0=rest,
                in1=rest,
                op=ALU.mult,
            )

        def divide(g, engine, rows=ALL_ROWS):
            if g not in h_grouped_of:
                h_grouped = handoff.tile([P, GROUP_ROWS, PACK], BF16, align_bytes=64)
                h_grouped_of[g] = h_grouped
            engine.tensor_tensor(
                out=h_grouped_of[g][:, rows, :].rearrange("p b (u e) -> p b u e", e=HALVES),
                in0=gated_of[g][:, :, rows, :].rearrange("p u b e -> p b u e"),
                in1=rden_of[g][:, :, rows, :].rearrange("p u b e -> p b u e"),
                op=ALU.mult,
            )

        def empty_share(g):
            out_sb = work.tile([P, GROUP_TILES, WIDTH], F32)
            out_sb_of[g] = out_sb
            nc.scalar.copy(out=out_sb[:, 1, VECTOR_COLUMNS:], in_=o_of[g, 1][:, VECTOR_COLUMNS:])

        def empty_out(g, j, engine, columns=slice(0, WIDTH)):
            if g not in out_sb_of:
                out_sb = work.tile([P, GROUP_TILES, WIDTH], F32)
                out_sb_of[g] = out_sb
            copy = nc.scalar.copy if engine is nc.scalar else nc.vector.tensor_copy
            copy(out=out_sb_of[g][:, j, columns], in_=o_of[g, j][:, columns])

        def store_out(g):
            nc.sync.dma_start(out=group_view(out, g), in_=out_sb_of[g][:])

        def store_tile(g, j):
            nc.sync.dma_start(out=group_view(out, g)[:, j, :], in_=out_sb_of[g][:, j, :])

        mix_bf = consts.tile([P, PACK], BF16)
        load_sx(0)
        nc.sync.dma_start(out=mix_bf[:], in_=time_mix_r[0].rearrange("(p t) -> p t", t=PACK))
        load_x(0)
        load_sx(1)
        load_den(0)
        load_x(1)
        wr_codes, wr_plane = load_weight(W_receptance_words, W_receptance_scales, "wr")
        load_sx(2)
        load_den(1)
        load_num(0)
        load_x(2)

        identity = consts.tile([P, P], F32)
        make_identity(nc, identity[:])
        half = consts.tile([P, 1], F32)
        nc.vector.memset(half[:], 0.5)
        mix_r = consts.tile([P, PACK], F32)
        nc.vector.tensor_copy(out=mix_r[:], in_=mix_bf[:])
        one_minus_mix = consts.tile([P, PACK], F32)
        nc.vector.tensor_scalar(
            out=one_minus_mix[:], in0=mix_bf[:], scalar1=-1.0, scalar2=1.0, op0=ALU.mult, op1=ALU.add
        )
        wr_sorted = consts.tile([P, WIDTH], U32, align_bytes=64)
        wr_sorted_plane = consts.tile([P, WIDTH], U8, align_bytes=64)

        def sort_receptance():
            nc.vector.tensor_copy(
                out=wr_sorted[:].bitcast(I32).rearrange("p (t m) -> p t m", t=PACK),
                in_=wr_codes[:].bitcast(I32).rearrange("p (m t) -> p t m", t=PACK),
            )
            nc.vector.tensor_copy(
                out=wr_sorted_plane[:].rearrange("p (t m) -> p m t", t=PACK),
                in_=wr_plane[:].rearrange("p (m t) -> p m t", t=PACK),
            )

        warm = consts.tile([P, 1], F32)
        for func in (ACT.Abs_reciprocal_sqrt, ACT.Relu, ACT.Square, ACT.Copy):
            nc.scalar.activation(out=warm[:], in_=half[:], func=func)

        def live(g):
            return 0 <= g < GROUPS

        for turn in range(-2, GROUPS):
            if live(turn - 3):
                quantise_h(turn - 3)
            if live(turn):
                quantise_xr(turn)
            if live(turn - 3):
                output_matmul(turn - 3, 0)
                output_matmul(turn - 3, 1)
            if live(turn):
                receptance_matmul(turn)
            if live(turn + 1):
                scale_state(turn + 1)
            if live(turn - 3):
                empty_share(turn - 3)
            if live(turn - 2):
                divide(turn - 2, nc.gpsimd)
            if live(turn - 1):
                gate_num(turn - 1)
            if live(turn):
                square_rsqrt(turn)
                square_rest(turn)
            if live(turn - 3):
                empty_out(turn - 3, 0, nc.vector)
            if live(turn + 1):
                transpose_den(turn + 1)
            if live(turn + 2):
                transpose_sx(turn + 2)
            if live(turn):
                transpose_num(turn)
                clip_below(turn)
            if live(turn + 1):
                mix_in_x(turn + 1)
            if live(turn + 2):
                transpose_x(turn + 2)
            if live(turn - 3):
                empty_out(turn - 3, 1, nc.vector, slice(0, VECTOR_COLUMNS))
            if live(turn + 1):
                regroup_xr(turn + 1)
                rsqrt_den(turn + 1)
            if turn == -1:
                sort_receptance()
            if live(turn + 2 + GROUPS_AHEAD):
                load_sx(turn + 2 + GROUPS_AHEAD)
                load_x(turn + 2 + GROUPS_AHEAD)
            if live(turn + 1 + GROUPS_AHEAD):
                load_den(turn + 1 + GROUPS_AHEAD)
            if live(turn + GROUPS_AHEAD):
                load_num(turn + GROUPS_AHEAD)
            if turn == -1:
                wo_codes, wo_plane = load_weight(W_output_words, W_output_scales, "wo")
            if live(turn - 3):
                store_out(turn - 3)

        last = GROUPS - 1
        tile_rows = [slice(j * P, (j + 1) * P) for j in range(GROUP_TILES)]

        def finish(g):
            for j in range(GROUP_TILES):
                output_matmul(g, j)
                empty_out(g, j, nc.scalar)
            store_out(g)

        quantise_h(last - 2)
        divide(last - 1, nc.vector, tile_rows[0])
        divide(last - 1, nc.gpsimd, tile_rows[1])
        gate_num(last, tile_rows[0])
        finish(last - 2)
        quantise_h(last - 1)
        divide(last, nc.vector, tile_rows[0])
        gate_num(last, tile_rows[1])
        finish(last - 1)
        quantise_h(last, tile_rows[0])
        divide(last, nc.vector, tile_rows[1])
        output_matmul(last, 0)
        empty_out(last, 0, nc.scalar)
        store_tile(last, 0)
        quantise_h(last, tile_rows[1])
        last_rows = slice(P, GROUP_ROWS)
        spare = gate_psum.tile([P, HALVES, GROUP_ROWS], F32, name="z")
        right = out_psum.tile([P, WIDTH], F32, name="o")
        for c, bank in enumerate((spare[:].rearrange("p e b -> p (e b)"), right[:])):
            columns = slice(c * WIDTH // 2, (c + 1) * WIDTH // 2)
            nc.tensor.matmul_mx(
                out=bank[:, : WIDTH // 2],
                lhsT=h_codes_of[last][:, last_rows].bitcast(FP8X4),
                lhsT_scale=h_scales_of[last][:, last_rows],
                rhs=wo_codes[:, c * PACK * WIDTH // 2 : (c + 1) * PACK * WIDTH // 2].bitcast(FP8X4),
                rhs_scale=wo_plane[:, columns],
                start=True,
                stop=True,
            )
            copy = nc.scalar.copy if c == 0 else nc.vector.tensor_copy
            copy(out=out_sb_of[last][:, 1, columns], in_=bank[:, : WIDTH // 2])
        store_tile(last, 1)
